import numpy as np
import ml_dtypes


def mxq(x, axis, fmt="e4m3"):
    dtype, down = {"e4m3": (ml_dtypes.float8_e4m3fn, 7), "e5m2": (ml_dtypes.float8_e5m2, 14)}[fmt]
    v = np.moveaxis(np.asarray(x, np.float32).astype(ml_dtypes.bfloat16).astype(np.float64), axis, -1)
    blocks = v.reshape(v.shape[:-1] + (-1, 32))
    amax = np.abs(blocks).max(-1, keepdims=True)
    byte = np.maximum(np.where(amax > 0, np.frexp(amax)[1] - 1 + 127, 0) - down, 1)
    scale = np.exp2(byte - 127.0)
    codes = (blocks / scale).astype(np.float32).astype(dtype).astype(np.float64)
    return np.moveaxis((codes * scale).reshape(v.shape), -1, axis)


WIDE = False


def mx_kscale(k):
    if not WIDE:
        return np.ones(k)
    levels = np.array([10, -10, 5, -5, 0])
    a = np.random.permutation(np.resize(levels, k // 512 * 4)).reshape(k // 512, 4)
    idx = np.arange(k)
    return np.exp2(a[idx // 512, idx % 128 // 32])


BF16 = ml_dtypes.bfloat16


def bf(x):
    return np.asarray(x, np.float32).astype(BF16)


def f64(x):
    return np.asarray(x).astype(np.float64)


B, S, D, H, KV, DH, W, KB = 1, 512, 2048, 16, 4, 128, 128, 512
THETA = 10000.0


def rotate_half(t):
    half = t.shape[-1] // 2
    return np.concatenate((-t[..., half:], t[..., :half]), axis=-1)


def rope_cos_sin():
    inv_freq = 1.0 / THETA ** (np.arange(0, DH, 2) / DH)
    ang = np.arange(S)[:, None] * inv_freq[None, :]
    cos = np.repeat(np.cos(ang), 2, axis=-1)[None, :, None, :]
    sin = np.repeat(np.sin(ang), 2, axis=-1)[None, :, None, :]
    return cos, sin


def setup_inputs():
    s = mx_kscale(D)
    return {"x": bf(np.random.standard_normal((B, S, D)) * s),
            "Wq": bf(np.random.standard_normal((D, H * DH)) / np.sqrt(D) / s[:, None]),
            "Wk": bf(np.random.standard_normal((D, KV * DH)) / np.sqrt(D) / s[:, None]),
            "Wv": bf(np.random.standard_normal((D, KV * DH)) * 1.5 / np.sqrt(D) / s[:, None])}


def reference(x, Wq, Wk, Wv):
    cos, sin = rope_cos_sin()
    xq = mxq(f64(x), 2, "e4m3")
    q = (xq @ mxq(f64(Wq), 0, "e4m3")).reshape(B, S, H, DH)
    k = (xq @ mxq(f64(Wk), 0, "e4m3")).reshape(B, S, KV, DH)
    v = (xq @ mxq(f64(Wv), 0, "e4m3")).reshape(B, S, KV, DH)
    q = q * cos + rotate_half(q) * sin
    k = k * cos + rotate_half(k) * sin
    return q.transpose(0, 2, 1, 3), k.transpose(0, 2, 1, 3), v.transpose(0, 2, 1, 3)

@@ -1,0 +1,210 @@
+import math
+from contextlib import ExitStack
+
+import concourse.masks as masks
+import concourse.mybir as mybir
+
+F32 = mybir.dt.float32
+BF16 = mybir.dt.bfloat16
+I32 = mybir.dt.int32
+U32 = mybir.dt.uint32
+U8 = mybir.dt.uint8
+FP8X4 = mybir.dt.float8_e4m3fn_x4
+ALU = mybir.AluOpType
+ACT = mybir.ActivationFunctionType
+
+P = 128
+S = 512
+D = 2048
+DH = 128
+T = S // P
+PACK = 4
+K_PASS = P * PACK
+PASSES = D // K_PASS
+NCOL = 512
+HPG = NCOL // DH
+NF = DH // 2
+THETA = 10000.0
+
+FLOPS = 2 * S * D * (2048 + 512 + 512)
+
+
+def build_tables(nc, const, cos_t, sin_t):
+    pos_i = const.tile([P, T, NF], I32)
+    nc.gpsimd.iota(pos_i[:], pattern=[[1, T], [0, NF]], base=0, channel_multiplier=T)
+    pos = const.tile([P, T, NF], F32)
+    nc.vector.tensor_copy(out=pos[:], in_=pos_i[:])
+    freq = const.tile([P, NF], F32)
+    nc.vector.memset(freq[:, 0:1], 1.0)
+    nc.vector.tensor_scalar(
+        out=freq[:, 0:1], in0=freq[:, 0:1], scalar1=1.0 / (2.0 * math.pi), scalar2=None, op0=ALU.mult
+    )
+    ratio = THETA ** (-1.0 / NF)
+    w = 1
+    while w < NF:
+        nc.vector.tensor_scalar(
+            out=freq[:, w : 2 * w], in0=freq[:, 0:w], scalar1=ratio**w, scalar2=None, op0=ALU.mult
+        )
+        w = 2 * w
+    turns = const.tile([P, 2, T, NF], F32)
+    nc.vector.tensor_tensor(
+        out=turns[:, 1], in0=pos[:], in1=freq[:].unsqueeze(1).to_broadcast([P, T, NF]), op=ALU.mult
+    )
+    nc.vector.tensor_scalar(out=turns[:, 0], in0=turns[:, 1], scalar1=0.25, scalar2=None, op0=ALU.add)
+    whole_i = const.tile([P, 2, T, NF], I32)
+    nc.vector.tensor_copy(out=whole_i[:], in_=turns[:])
+    whole = const.tile([P, 2, T, NF], F32)
+    nc.vector.tensor_copy(out=whole[:], in_=whole_i[:])
+    frac = const.tile([P, 2, T, NF], F32)
+    nc.vector.tensor_tensor(out=frac[:], in0=turns[:], in1=whole[:], op=ALU.subtract)
+    neg = const.tile([P, 2, T, NF], F32)
+    flat = "p a t m -> p (a t m)"
+    nc.vector.scalar_tensor_tensor(
+        out=neg[:].rearrange(flat),
+        in0=frac[:].rearrange(flat),
+        scalar=0.5,
+        in1=frac[:].rearrange(flat),
+        op0=ALU.is_gt,
+        op1=ALU.subtract,
+    )
+    two_pi = 2.0 * math.pi
+    nc.scalar.activation(
+        out=cos_t[:].rearrange("p t (m e) -> p t m e", e=2),
+        in_=neg[:, 0].unsqueeze(3).to_broadcast([P, T, NF, 2]),
+        func=ACT.Sin,
+        scale=-two_pi,
+    )
+    half = NF // 2
+    for a in range(2):
+        nc.scalar.activation(
+            out=sin_t[:, :, a * NF : (a + 1) * NF].rearrange("p t (m e) -> p t m e", e=2),
+            in_=neg[:, 1, :, a * half : (a + 1) * half].unsqueeze(3).to_broadcast([P, T, half, 2]),
+            func=ACT.Sin,
+            scale=two_pi if a == 0 else -two_pi,
+        )
+
+
+def tile_spikinggroupedslidingattention_pa_kernel(tc, x, Wq, Wk, Wv, out_0, out_1, out_2):
+    nc = tc.nc
+    with ExitStack() as ctx:
+        const = ctx.enter_context(tc.tile_pool(name="const", bufs=1))
+        xpool = ctx.enter_context(tc.tile_pool(name="xpool", bufs=1))
+        xgp = ctx.enter_context(tc.tile_pool(name="xgp", bufs=2))
+        rawp = ctx.enter_context(tc.tile_pool(name="rawp", bufs=10))
+        grpp = ctx.enter_context(tc.tile_pool(name="grpp", bufs=4))
+        wcp = ctx.enter_context(tc.tile_pool(name="wcp", bufs=3))
+        prodp = ctx.enter_context(tc.tile_pool(name="prodp", bufs=4))
+        outp = ctx.enter_context(tc.tile_pool(name="outp", bufs=3))
+        psum = ctx.enter_context(tc.psum_pool(name="psum", bufs=8))
+
+        x_v = x.rearrange("b (p t) k -> p (b t) k", t=T)
+        x_sb = xpool.tile([P, T, D], BF16)
+        for t in range(T):
+            nc.sync.dma_start(out=x_sb[:, t, :], in_=x_v[:, t, :])
+
+        cos_t = const.tile([P, T, DH], F32)
+        sin_t = const.tile([P, T, DH], F32)
+        build_tables(nc, const, cos_t, sin_t)
+
+        ident = const.tile([P, P], F32)
+        masks.make_identity(nc, ident[:])
+
+        xc = xpool.tile([P, T, PASSES, P], U32, align_bytes=64)
+        xs = xpool.tile([P, T, PASSES, P], U8, align_bytes=64)
+        n_copy = 0
+        for t in range(T):
+            words = x_sb[:, t, :].bitcast(F32).rearrange("p (g q u) -> p g q u", g=PASSES, u=2)
+            xg = xgp.tile([P, PASSES * P * PACK], BF16, align_bytes=64)
+            xg_w = xg[:].bitcast(F32).rearrange("p (g r u) -> p g r u", g=PASSES, u=2)
+            for gp in range(PASSES // 2):
+                xt = psum.tile([P, 4, P], F32, tag="acc")
+                for gl in range(2):
+                    for u in range(2):
+                        nc.tensor.transpose(xt[:, 2 * gl + u, :], words[:, 2 * gp + gl, :, u], ident[:])
+                src = xt[:].rearrange("p (g u) r -> p g r u", u=2)
+                dst = xg_w[:, 2 * gp : 2 * gp + 2]
+                if n_copy % 2 == 0:
+                    nc.scalar.copy(out=dst, in_=src)
+                else:
+                    nc.vector.tensor_copy(out=dst, in_=src)
+                n_copy += 1
+            nc.vector.quantize_mx(
+                out=xc[:, t].rearrange("p g r -> p (g r)").bitcast(FP8X4),
+                scales=xs[:, t].rearrange("p g r -> p (g r)"),
+                in_=xg[:],
+            )
+
+        groups = [(Wk, 0, out_1, 0, True)]
+        for q in range(4):
+            groups.append((Wq, q * NCOL, out_0, q * HPG, True))
+        groups.append((Wv, 0, out_2, 0, False))
+
+        for w_dram, c0, out_dram, h0, rope in groups:
+            wc = wcp.tile([P, PASSES, NCOL], U32, align_bytes=64)
+            ws = wcp.tile([P, PASSES, NCOL], U8, align_bytes=64)
+            for g in range(PASSES):
+                raw = rawp.tile([P, PACK, NCOL], BF16)
+                nc.sync.dma_start(
+                    out=raw[:],
+                    in_=w_dram[g * K_PASS : (g + 1) * K_PASS, c0 : c0 + NCOL].rearrange("(p j) c -> p j c", j=PACK),
+                )
+                grp = grpp.tile([P, NCOL, PACK], BF16, align_bytes=64)
+                dst = grp[:].rearrange("p (c i) j -> p c j i", i=4)
+                src = raw[:].rearrange("p j (c i) -> p c j i", i=4)
+                on_vector = (g == 3) if rope else (g % 2 == 1)
+                if on_vector:
+                    nc.vector.tensor_copy(out=dst, in_=src)
+                else:
+                    nc.scalar.copy(out=dst, in_=src)
+                nc.vector.quantize_mx(
+                    out=wc[:, g, :].bitcast(FP8X4),
+                    scales=ws[:, g, :],
+                    in_=grp[:].rearrange("p c j -> p (c j)"),
+                )
+            accs = []
+            for t in range(T):
+                acc = psum.tile([P, NCOL], F32, tag="acc", name="acc")
+                accs.append(acc)
+            for g in range(PASSES):
+                for t in range(T):
+                    nc.tensor.matmul_mx(
+                        out=accs[t][:],
+                        lhsT=xc[:, t, g, :].bitcast(FP8X4),
+                        lhsT_scale=xs[:, t, g, :],
+                        rhs=wc[:, g, :].bitcast(FP8X4),
+                        rhs_scale=ws[:, g, :],
+                        start=(g == 0),
+                        stop=(g == PASSES - 1),
+                    )
+            out_sb = outp.tile([P, HPG, T, DH], F32)
+            for t in range(T):
+                acc_h = accs[t][:].rearrange("p (h i) -> p h i", i=DH)
+                if not rope:
+                    if t % 2 == 0:
+                        nc.scalar.copy(out=out_sb[:, :, t, :], in_=acc_h)
+                    else:
+                        nc.vector.tensor_copy(out=out_sb[:, :, t, :], in_=acc_h)
+                    continue
+                tq = prodp.tile([P, HPG, DH], F32)
+                uq = prodp.tile([P, HPG, DH], F32)
+                nc.vector.tensor_tensor(
+                    out=tq[:],
+                    in0=acc_h,
+                    in1=cos_t[:, t, :].unsqueeze(1).to_broadcast([P, HPG, DH]),
+                    op=ALU.mult,
+                )
+                hw = DH // 2
+                for a in range(2):
+                    nc.vector.tensor_tensor(
+                        out=uq[:, :, a * hw : (a + 1) * hw],
+                        in0=acc_h[:, :, (1 - a) * hw : (2 - a) * hw],
+                        in1=sin_t[:, t, a * hw : (a + 1) * hw].unsqueeze(1).to_broadcast([P, HPG, hw]),
+                        op=ALU.mult,
+                    )
+                nc.gpsimd.tensor_tensor(out=out_sb[:, :, t, :], in0=tq[:], in1=uq[:], op=ALU.add)
+            dst = out_dram.rearrange("b h (p t) i -> p (b h) (t i)", t=T)[:, h0 : h0 + HPG, :]
+            src = out_sb[:].rearrange("p h t i -> p h (t i)")
+            if rope:
+                nc.gpsimd.dma_start(out=dst, in_=src)
+            else:
+                nc.sync.dma_start(out=dst, in_=src)

@@ -68,13 +68,21 @@ def build_tables(nc, const, cos_t, sin_t):
         op1=ALU.subtract,
     )
     two_pi = 2.0 * math.pi
+    half = NF // 2
+
+    def sines():
+        sine_calls(nc, cos_t, sin_t, neg, two_pi, half)
+
+    return sines
+
+
+def sine_calls(nc, cos_t, sin_t, neg, two_pi, half):
     nc.scalar.activation(
         out=cos_t[:].rearrange("p t (m e) -> p t m e", e=2),
         in_=neg[:, 0].unsqueeze(3).to_broadcast([P, T, NF, 2]),
         func=ACT.Sin,
         scale=-two_pi,
     )
-    half = NF // 2
     for a in range(2):
         nc.scalar.activation(
             out=sin_t[:, :, a * NF : (a + 1) * NF].rearrange("p t (m e) -> p t m e", e=2),
@@ -84,127 +92,202 @@ def build_tables(nc, const, cos_t, sin_t):
         )
 
 
+N_UNITS = 24
+N_GROUPS = 6
+LOOKAHEAD = 10
+RAW_BUFS = 12
+ON_VECTOR = (1, 3, 9, 15, 21, 23)
+HEAD_LOADS = ("u0", "u1", "x0", "u2", "x1", "u3", "x2", "u4", "x3", "u5", "u6", "u7", "u8", "u9")
+
+
 def tile_spikinggroupedslidingattention_pa_kernel(tc, x, Wq, Wk, Wv, out_0, out_1, out_2):
     nc = tc.nc
     with ExitStack() as ctx:
         const = ctx.enter_context(tc.tile_pool(name="const", bufs=1))
         xpool = ctx.enter_context(tc.tile_pool(name="xpool", bufs=1))
         xgp = ctx.enter_context(tc.tile_pool(name="xgp", bufs=2))
-        rawp = ctx.enter_context(tc.tile_pool(name="rawp", bufs=10))
-        grpp = ctx.enter_context(tc.tile_pool(name="grpp", bufs=4))
+        rawp = ctx.enter_context(tc.tile_pool(name="rawp", bufs=RAW_BUFS))
+        grpp = ctx.enter_context(tc.tile_pool(name="grpp", bufs=3))
         wcp = ctx.enter_context(tc.tile_pool(name="wcp", bufs=3))
-        prodp = ctx.enter_context(tc.tile_pool(name="prodp", bufs=4))
+        prodp = ctx.enter_context(tc.tile_pool(name="prodp", bufs=3))
         outp = ctx.enter_context(tc.tile_pool(name="outp", bufs=3))
         psum = ctx.enter_context(tc.psum_pool(name="psum", bufs=8))
-
-        x_v = x.rearrange("b (p t) k -> p (b t) k", t=T)
-        x_sb = xpool.tile([P, T, D], BF16)
-        for t in range(T):
-            nc.sync.dma_start(out=x_sb[:, t, :], in_=x_v[:, t, :])
-
-        cos_t = const.tile([P, T, DH], F32)
-        sin_t = const.tile([P, T, DH], F32)
-        build_tables(nc, const, cos_t, sin_t)
-
-        ident = const.tile([P, P], F32)
-        masks.make_identity(nc, ident[:])
-
-        xc = xpool.tile([P, T, PASSES, P], U32, align_bytes=64)
-        xs = xpool.tile([P, T, PASSES, P], U8, align_bytes=64)
-        n_copy = 0
-        for t in range(T):
-            words = x_sb[:, t, :].bitcast(F32).rearrange("p (g q u) -> p g q u", g=PASSES, u=2)
-            xg = xgp.tile([P, PASSES * P * PACK], BF16, align_bytes=64)
-            xg_w = xg[:].bitcast(F32).rearrange("p (g r u) -> p g r u", g=PASSES, u=2)
-            for gp in range(PASSES // 2):
-                xt = psum.tile([P, 4, P], F32, tag="acc")
-                for gl in range(2):
-                    for u in range(2):
-                        nc.tensor.transpose(xt[:, 2 * gl + u, :], words[:, 2 * gp + gl, :, u], ident[:])
-                src = xt[:].rearrange("p (g u) r -> p g r u", u=2)
-                dst = xg_w[:, 2 * gp : 2 * gp + 2]
-                if n_copy % 2 == 0:
-                    nc.scalar.copy(out=dst, in_=src)
-                else:
-                    nc.vector.tensor_copy(out=dst, in_=src)
-                n_copy += 1
-            nc.vector.quantize_mx(
-                out=xc[:, t].rearrange("p g r -> p (g r)").bitcast(FP8X4),
-                scales=xs[:, t].rearrange("p g r -> p (g r)"),
-                in_=xg[:],
-            )
+        ctx.enter_context(tc.manual_schedule())
 
         groups = [(Wk, 0, out_1, 0, True)]
         for q in range(4):
             groups.append((Wq, q * NCOL, out_0, q * HPG, True))
         groups.append((Wv, 0, out_2, 0, False))
 
-        for w_dram, c0, out_dram, h0, rope in groups:
-            wc = wcp.tile([P, PASSES, NCOL], U32, align_bytes=64)
-            ws = wcp.tile([P, PASSES, NCOL], U8, align_bytes=64)
-            for g in range(PASSES):
-                raw = rawp.tile([P, PACK, NCOL], BF16)
-                nc.sync.dma_start(
-                    out=raw[:],
-                    in_=w_dram[g * K_PASS : (g + 1) * K_PASS, c0 : c0 + NCOL].rearrange("(p j) c -> p j c", j=PACK),
-                )
-                grp = grpp.tile([P, NCOL, PACK], BF16, align_bytes=64)
-                dst = grp[:].rearrange("p (c i) j -> p c j i", i=4)
-                src = raw[:].rearrange("p j (c i) -> p c j i", i=4)
-                on_vector = (g == 3) if rope else (g % 2 == 1)
-                if on_vector:
-                    nc.vector.tensor_copy(out=dst, in_=src)
-                else:
+        x_v = x.rearrange("b (p t) k -> p (b t) k", t=T)
+        x_sb = xpool.tile([P, T, D], BF16)
+        xc = xpool.tile([P, T, PASSES, P], U32, align_bytes=64)
+        xs = xpool.tile([P, T, PASSES, P], U8, align_bytes=64)
+        cos_t = const.tile([P, T, DH], F32)
+        sin_t = const.tile([P, T, DH], F32)
+        ident = const.tile([P, P], F32)
+
+        raw = {}
+        grp = {}
+        codes = {}
+        accs = {}
+        outs = {}
+        prods = {}
+        xts = {}
+        xgs = {}
+
+        def load_unit(u):
+            w_dram, c0 = groups[u // PASSES][0:2]
+            g = u % PASSES
+            raw[u] = rawp.tile([P, PACK, NCOL], BF16, name="raw")
+            nc.sync.dma_start(
+                out=raw[u][:],
+                in_=w_dram[g * K_PASS : (g + 1) * K_PASS, c0 : c0 + NCOL].rearrange("(p j) c -> p j c", j=PACK),
+            )
+
+        def load_x(t):
+            nc.sync.dma_start(out=x_sb[:, t, :], in_=x_v[:, t, :])
+
+        def x_transposes(t):
+            words = x_sb[:, t, :].bitcast(F32).rearrange("p (g q u) -> p g q u", g=PASSES, u=2)
+            for gp in range(PASSES // 2):
+                xt = psum.tile([P, 4, P], F32, tag="acc", name="xt")
+                xts[(t, gp)] = xt
+                for gl in range(2):
+                    for u in range(2):
+                        nc.tensor.transpose(xt[:, 2 * gl + u, :], words[:, 2 * gp + gl, :, u], ident[:])
+
+        def x_copies(t):
+            xgs[t] = xgp.tile([P, PASSES * P * PACK], BF16, align_bytes=64, name="xg")
+            xg_w = xgs[t][:].bitcast(F32).rearrange("p (g r u) -> p g r u", g=PASSES, u=2)
+            for gp in range(PASSES // 2):
+                src = xts[(t, gp)][:].rearrange("p (g u) r -> p g r u", u=2)
+                dst = xg_w[:, 2 * gp : 2 * gp + 2]
+                if gp == 0:
                     nc.scalar.copy(out=dst, in_=src)
-                nc.vector.quantize_mx(
-                    out=wc[:, g, :].bitcast(FP8X4),
-                    scales=ws[:, g, :],
-                    in_=grp[:].rearrange("p c j -> p (c j)"),
-                )
-            accs = []
-            for t in range(T):
-                acc = psum.tile([P, NCOL], F32, tag="acc", name="acc")
-                accs.append(acc)
+                else:
+                    nc.vector.tensor_copy(out=dst, in_=src)
+
+        def x_quant(t):
+            nc.vector.quantize_mx(
+                out=xc[:, t].rearrange("p g r -> p (g r)").bitcast(FP8X4),
+                scales=xs[:, t].rearrange("p g r -> p (g r)"),
+                in_=xgs[t][:],
+            )
+
+        def regroup(u):
+            grp[u] = grpp.tile([P, NCOL * PACK], BF16, align_bytes=64, name="grp")
+            dst = grp[u][:].rearrange("p (c i j) -> p c j i", i=4, j=PACK)
+            src = raw[u][:].rearrange("p j (c i) -> p c j i", i=4)
+            if u in ON_VECTOR:
+                nc.vector.tensor_copy(out=dst, in_=src)
+            else:
+                nc.scalar.copy(out=dst, in_=src)
+
+        def quant(u):
+            n = u // PASSES
+            g = u % PASSES
+            if g == 0:
+                wc = wcp.tile([P, PASSES, NCOL], U32, align_bytes=64, name="wc")
+                ws = wcp.tile([P, PASSES, NCOL], U8, align_bytes=64, name="ws")
+                codes[n] = (wc, ws)
+            wc, ws = codes[n]
+            nc.vector.quantize_mx(out=wc[:, g, :].bitcast(FP8X4), scales=ws[:, g, :], in_=grp[u][:])
+
+        def mx_pass(n, t, g):
+            wc, ws = codes[n]
+            nc.tensor.matmul_mx(
+                out=accs[(n, t)][:],
+                lhsT=xc[:, t, g, :].bitcast(FP8X4),
+                lhsT_scale=xs[:, t, g, :],
+                rhs=wc[:, g, :].bitcast(FP8X4),
+                rhs_scale=ws[:, g, :],
+                start=(g == 0),
+                stop=(g == PASSES - 1),
+            )
+
+        def mx_tile(v):
+            n = v // T
+            t = v % T
+            accs[(n, t)] = psum.tile([P, NCOL], F32, tag="acc", name="acc")
             for g in range(PASSES):
-                for t in range(T):
-                    nc.tensor.matmul_mx(
-                        out=accs[t][:],
-                        lhsT=xc[:, t, g, :].bitcast(FP8X4),
-                        lhsT_scale=xs[:, t, g, :],
-                        rhs=wc[:, g, :].bitcast(FP8X4),
-                        rhs_scale=ws[:, g, :],
-                        start=(g == 0),
-                        stop=(g == PASSES - 1),
-                    )
-            out_sb = outp.tile([P, HPG, T, DH], F32)
+                mx_pass(n, t, g)
+
+        def mx_unit(u):
+            n = u // PASSES
+            g = u % PASSES
             for t in range(T):
-                acc_h = accs[t][:].rearrange("p (h i) -> p h i", i=DH)
-                if not rope:
-                    if t % 2 == 0:
-                        nc.scalar.copy(out=out_sb[:, :, t, :], in_=acc_h)
-                    else:
-                        nc.vector.tensor_copy(out=out_sb[:, :, t, :], in_=acc_h)
-                    continue
-                tq = prodp.tile([P, HPG, DH], F32)
-                uq = prodp.tile([P, HPG, DH], F32)
+                if g == 0:
+                    accs[(n, t)] = psum.tile([P, NCOL], F32, tag="acc", name="acc")
+                mx_pass(n, t, g)
+
+        def rope(v):
+            n = v // T
+            t = v % T
+            if t == 0:
+                outs[n] = outp.tile([P, HPG, T, DH], F32, name="out_sb")
+            acc_h = accs[(n, t)][:].rearrange("p (h i) -> p h i", i=DH)
+            uq = prodp.tile([P, HPG, DH], F32, name="uq")
+            hw = DH // 2
+            for a in range(2):
                 nc.vector.tensor_tensor(
-                    out=tq[:],
-                    in0=acc_h,
-                    in1=cos_t[:, t, :].unsqueeze(1).to_broadcast([P, HPG, DH]),
+                    out=uq[:, :, a * hw : (a + 1) * hw],
+                    in0=acc_h[:, :, (1 - a) * hw : (2 - a) * hw],
+                    in1=sin_t[:, t, a * hw : (a + 1) * hw].unsqueeze(1).to_broadcast([P, HPG, hw]),
                     op=ALU.mult,
                 )
-                hw = DH // 2
-                for a in range(2):
-                    nc.vector.tensor_tensor(
-                        out=uq[:, :, a * hw : (a + 1) * hw],
-                        in0=acc_h[:, :, (1 - a) * hw : (2 - a) * hw],
-                        in1=sin_t[:, t, a * hw : (a + 1) * hw].unsqueeze(1).to_broadcast([P, HPG, hw]),
-                        op=ALU.mult,
-                    )
-                nc.gpsimd.tensor_tensor(out=out_sb[:, :, t, :], in0=tq[:], in1=uq[:], op=ALU.add)
-            dst = out_dram.rearrange("b h (p t) i -> p (b h) (t i)", t=T)[:, h0 : h0 + HPG, :]
-            src = out_sb[:].rearrange("p h t i -> p h (t i)")
-            if rope:
-                nc.gpsimd.dma_start(out=dst, in_=src)
+            nc.vector.tensor_tensor(
+                out=outs[n][:, :, t, :],
+                in0=acc_h,
+                in1=cos_t[:, t, :].unsqueeze(1).to_broadcast([P, HPG, DH]),
+                op=ALU.mult,
+            )
+            nc.gpsimd.tensor_tensor(out=outs[n][:, :, t, :], in0=outs[n][:, :, t, :], in1=uq[:], op=ALU.add)
+
+        def store(n):
+            out_dram, h0 = groups[n][2:4]
+            nc.sync.dma_start(
+                out=out_dram.rearrange("b h (p t) i -> p (b h) (t i)", t=T)[:, h0 : h0 + HPG, :],
+                in_=outs[n][:].rearrange("p h t i -> p h (t i)"),
+            )
+
+        for item in HEAD_LOADS:
+            if item[0] == "u":
+                load_unit(int(item[1:]))
             else:
-                nc.sync.dma_start(out=dst, in_=src)
+                load_x(int(item[1:]))
+        tables = build_tables(nc, const, cos_t, sin_t)
+        masks.make_identity(nc, ident[:])
+
+        last = N_GROUPS - 1
+        for k in range(N_UNITS + 2):
+            if LOOKAHEAD <= k + LOOKAHEAD < N_UNITS:
+                load_unit(k + LOOKAHEAD)
+            if 0 <= k - 1 < T:
+                x_transposes(k - 1)
+            if 0 <= k - 1 < T:
+                x_copies(k - 1)
+            if k < N_UNITS:
+                regroup(k)
+            if k == 1:
+                tables()
+            if 0 <= k - 1 < N_UNITS:
+                quant(k - 1)
+            if 0 <= k - 2 < T:
+                x_quant(k - 2)
+            if 0 <= k - 4 < last * T:
+                mx_tile(k - 4)
+            if last * PASSES <= k - 1 < N_UNITS:
+                mx_unit(k - 1)
+            if 0 <= k - 5 < last * T:
+                rope(k - 5)
+                if (k - 5) % T == T - 1:
+                    store((k - 5) // T)
+        outs[last] = outp.tile([P, HPG, T, DH], F32, name="out_sb")
+        for t in range(T):
+            acc_h = accs[(last, t)][:].rearrange("p (h i) -> p h i", i=DH)
+            if t % 2 == 0:
+                nc.scalar.copy(out=outs[last][:, :, t, :], in_=acc_h)
+            else:
+                nc.vector.tensor_copy(out=outs[last][:, :, t, :], in_=acc_h)
+        store(last)

@@ -32,10 +32,11 @@ FLOPS = 2 * S * D * (2048 + 512 + 512)
 def build_tables(nc, const, cos_t, sin_t):
     pos_i = const.tile([P, T, NF], I32)
     nc.gpsimd.iota(pos_i[:], pattern=[[1, T], [0, NF]], base=0, channel_multiplier=T)
-    pos = const.tile([P, T, NF], F32)
-    nc.vector.tensor_copy(out=pos[:], in_=pos_i[:])
     freq = const.tile([P, NF], F32)
     nc.vector.memset(freq[:, 0:1], 1.0)
+    warm = const.tile([P, 2], F32)
+    nc.vector.memset(warm[:, 0:1], 0.0)
+    nc.scalar.activation(out=warm[:, 1:2], in_=warm[:, 0:1], func=ACT.Sin)
     nc.vector.tensor_scalar(
         out=freq[:, 0:1], in0=freq[:, 0:1], scalar1=1.0 / (2.0 * math.pi), scalar2=None, op0=ALU.mult
     )
@@ -46,6 +47,8 @@ def build_tables(nc, const, cos_t, sin_t):
             out=freq[:, w : 2 * w], in0=freq[:, 0:w], scalar1=ratio**w, scalar2=None, op0=ALU.mult
         )
         w = 2 * w
+    pos = const.tile([P, T, NF], F32)
+    nc.vector.tensor_copy(out=pos[:], in_=pos_i[:])
     turns = const.tile([P, 2, T, NF], F32)
     nc.vector.tensor_tensor(
         out=turns[:, 1], in0=pos[:], in1=freq[:].unsqueeze(1).to_broadcast([P, T, NF]), op=ALU.mult
@@ -94,10 +97,10 @@ def sine_calls(nc, cos_t, sin_t, neg, two_pi, half):
 
 N_UNITS = 24
 N_GROUPS = 6
-LOOKAHEAD = 10
-RAW_BUFS = 12
-ON_VECTOR = (1, 3, 9, 15, 21, 23)
-HEAD_LOADS = ("u0", "u1", "x0", "u2", "x1", "u3", "x2", "u4", "x3", "u5", "u6", "u7", "u8", "u9")
+LOOKAHEAD = 12
+RAW_BUFS = 14
+ON_VECTOR = (1, 3, 8, 12, 16, 20)
+HEAD_LOADS = ("u0", "u1", "x0", "u2", "x1", "u3", "x2", "u4", "x3", "u5", "u6", "u7", "u8", "u9", "u10", "u11")
 
 
 def tile_spikinggroupedslidingattention_pa_kernel(tc, x, Wq, Wk, Wv, out_0, out_1, out_2):
@@ -112,7 +115,6 @@ def tile_spikinggroupedslidingattention_pa_kernel(tc, x, Wq, Wk, Wv, out_0, out_
         prodp = ctx.enter_context(tc.tile_pool(name="prodp", bufs=3))
         outp = ctx.enter_context(tc.tile_pool(name="outp", bufs=3))
         psum = ctx.enter_context(tc.psum_pool(name="psum", bufs=8))
-        ctx.enter_context(tc.manual_schedule())
 
         groups = [(Wk, 0, out_1, 0, True)]
         for q in range(4):
@@ -163,10 +165,7 @@ def tile_spikinggroupedslidingattention_pa_kernel(tc, x, Wq, Wk, Wv, out_0, out_
             for gp in range(PASSES // 2):
                 src = xts[(t, gp)][:].rearrange("p (g u) r -> p g r u", u=2)
                 dst = xg_w[:, 2 * gp : 2 * gp + 2]
-                if gp == 0:
-                    nc.scalar.copy(out=dst, in_=src)
-                else:
-                    nc.vector.tensor_copy(out=dst, in_=src)
+                nc.scalar.copy(out=dst, in_=src)
 
         def x_quant(t):
             nc.vector.quantize_mx(
@@ -251,6 +250,13 @@ def tile_spikinggroupedslidingattention_pa_kernel(tc, x, Wq, Wk, Wv, out_0, out_
                 in_=outs[n][:].rearrange("p h t i -> p h (t i)"),
             )
 
+        def store_tile(n, t):
+            out_dram, h0 = groups[n][2:4]
+            nc.sync.dma_start(
+                out=out_dram.rearrange("b h (p t) i -> p t (b h) i", t=T)[:, t, h0 : h0 + HPG, :],
+                in_=outs[n][:, :, t, :],
+            )
+
         for item in HEAD_LOADS:
             if item[0] == "u":
                 load_unit(int(item[1:]))
@@ -281,13 +287,12 @@ def tile_spikinggroupedslidingattention_pa_kernel(tc, x, Wq, Wk, Wv, out_0, out_
                 mx_unit(k - 1)
             if 0 <= k - 5 < last * T:
                 rope(k - 5)
-                if (k - 5) % T == T - 1:
+                if (k - 5) // T == last - 1:
+                    store_tile(last - 1, (k - 5) % T)
+                elif (k - 5) % T == T - 1:
                     store((k - 5) // T)
         outs[last] = outp.tile([P, HPG, T, DH], F32, name="out_sb")
         for t in range(T):
             acc_h = accs[(last, t)][:].rearrange("p (h i) -> p h i", i=DH)
-            if t % 2 == 0:
-                nc.scalar.copy(out=outs[last][:, :, t, :], in_=acc_h)
-            else:
-                nc.vector.tensor_copy(out=outs[last][:, :, t, :], in_=acc_h)
-        store(last)
+            nc.scalar.copy(out=outs[last][:, :, t, :], in_=acc_h)
+            store_tile(last, t)

@@ -99,7 +99,8 @@ N_UNITS = 24
 N_GROUPS = 6
 LOOKAHEAD = 12
 RAW_BUFS = 14
-ON_VECTOR = (1, 3, 8, 12, 16, 20)
+ON_VECTOR = (1, 3, 12)
+ASSISTED = (5, 7, 9, 11, 14, 16, 18, 20, 22)
 HEAD_LOADS = ("u0", "u1", "x0", "u2", "x1", "u3", "x2", "u4", "x3", "u5", "u6", "u7", "u8", "u9", "u10", "u11")
 
 
@@ -114,7 +115,8 @@ def tile_spikinggroupedslidingattention_pa_kernel(tc, x, Wq, Wk, Wv, out_0, out_
         wcp = ctx.enter_context(tc.tile_pool(name="wcp", bufs=3))
         prodp = ctx.enter_context(tc.tile_pool(name="prodp", bufs=3))
         outp = ctx.enter_context(tc.tile_pool(name="outp", bufs=3))
-        psum = ctx.enter_context(tc.psum_pool(name="psum", bufs=8))
+        psum = ctx.enter_context(tc.psum_pool(name="psum", bufs=6))
+        psum_b = ctx.enter_context(tc.psum_pool(name="psum_b", bufs=2))
 
         groups = [(Wk, 0, out_1, 0, True)]
         for q in range(4):
@@ -128,6 +130,7 @@ def tile_spikinggroupedslidingattention_pa_kernel(tc, x, Wq, Wk, Wv, out_0, out_
         cos_t = const.tile([P, T, DH], F32)
         sin_t = const.tile([P, T, DH], F32)
         ident = const.tile([P, P], F32)
+        ident_b = const.tile([P, P], BF16)
 
         raw = {}
         grp = {}
@@ -174,8 +177,30 @@ def tile_spikinggroupedslidingattention_pa_kernel(tc, x, Wq, Wk, Wv, out_0, out_
                 in_=xgs[t][:],
             )
 
+        def assist(u):
+            hc = NCOL // 2
+            for hh in range(2):
+                pb = psum_b.tile([P, hc, PACK], BF16, name="pb")
+                xts[("pb", u, hh)] = pb
+                for jp in range(PACK // 2):
+                    nc.tensor.matmul(
+                        out=pb[:, :, 2 * jp : 2 * jp + 2],
+                        lhsT=ident_b[:],
+                        rhs=raw[u][:, 2 * jp : 2 * jp + 2, hh * hc : (hh + 1) * hc].rearrange("p j c -> p c j"),
+                        start=True,
+                        stop=True,
+                    )
+
         def regroup(u):
             grp[u] = grpp.tile([P, NCOL * PACK], BF16, align_bytes=64, name="grp")
+            if u in ASSISTED:
+                half = NCOL * PACK // 2
+                for hh in range(2):
+                    nc.scalar.copy(
+                        out=grp[u][:, hh * half : (hh + 1) * half],
+                        in_=xts[("pb", u, hh)][:].rearrange("p c j -> p (c j)"),
+                    )
+                return
             dst = grp[u][:].rearrange("p (c i j) -> p c j i", i=4, j=PACK)
             src = raw[u][:].rearrange("p j (c i) -> p c j i", i=4)
             if u in ON_VECTOR:
@@ -264,6 +289,7 @@ def tile_spikinggroupedslidingattention_pa_kernel(tc, x, Wq, Wk, Wv, out_0, out_
                 load_x(int(item[1:]))
         tables = build_tables(nc, const, cos_t, sin_t)
         masks.make_identity(nc, ident[:])
+        masks.make_identity(nc, ident_b[:])
 
         last = N_GROUPS - 1
         for k in range(N_UNITS + 2):
@@ -271,6 +297,8 @@ def tile_spikinggroupedslidingattention_pa_kernel(tc, x, Wq, Wk, Wv, out_0, out_
                 load_unit(k + LOOKAHEAD)
             if 0 <= k - 1 < T:
                 x_transposes(k - 1)
+            if k + 1 in ASSISTED:
+                assist(k + 1)
             if 0 <= k - 1 < T:
                 x_copies(k - 1)
             if k < N_UNITS:

@@ -17,26 +17,30 @@ P = 128
 S = 512
 D = 2048
 DH = 128
+HALF = DH // 2
+NF = DH // 2
+THETA = 10000.0
 T = S // P
 PACK = 4
 K_PASS = P * PACK
 PASSES = D // K_PASS
 NCOL = 512
 HPG = NCOL // DH
-NF = DH // 2
-THETA = 10000.0
+N_GROUPS = 6
+N_UNITS = N_GROUPS * PASSES
+LOOKAHEAD = 12
+RAW_BUFS = LOOKAHEAD + 2
 
 FLOPS = 2 * S * D * (2048 + 512 + 512)
 
 
-def build_tables(nc, const, cos_t, sin_t):
-    pos_i = const.tile([P, T, NF], I32)
-    nc.gpsimd.iota(pos_i[:], pattern=[[1, T], [0, NF]], base=0, channel_multiplier=T)
-    freq = const.tile([P, NF], F32)
-    nc.vector.memset(freq[:, 0:1], 1.0)
-    warm = const.tile([P, 2], F32)
+def rope_tables(nc, pool, cos_t, sin_t):
+    warm = pool.tile([P, 2], F32)
     nc.vector.memset(warm[:, 0:1], 0.0)
     nc.scalar.activation(out=warm[:, 1:2], in_=warm[:, 0:1], func=ACT.Sin)
+
+    freq = pool.tile([P, NF], F32)
+    nc.vector.memset(freq[:, 0:1], 1.0)
     nc.vector.tensor_scalar(
         out=freq[:, 0:1], in0=freq[:, 0:1], scalar1=1.0 / (2.0 * math.pi), scalar2=None, op0=ALU.mult
     )
@@ -47,99 +51,84 @@ def build_tables(nc, const, cos_t, sin_t):
             out=freq[:, w : 2 * w], in0=freq[:, 0:w], scalar1=ratio**w, scalar2=None, op0=ALU.mult
         )
         w = 2 * w
-    pos = const.tile([P, T, NF], F32)
+
+    pos_i = pool.tile([P, T, NF], I32)
+    nc.gpsimd.iota(pos_i[:], pattern=[[1, T], [0, NF]], base=0, channel_multiplier=T)
+    pos = pool.tile([P, T, NF], F32)
     nc.vector.tensor_copy(out=pos[:], in_=pos_i[:])
-    turns = const.tile([P, 2, T, NF], F32)
+
+    turns = pool.tile([P, 2, T, NF], F32)
     nc.vector.tensor_tensor(
         out=turns[:, 1], in0=pos[:], in1=freq[:].unsqueeze(1).to_broadcast([P, T, NF]), op=ALU.mult
     )
     nc.vector.tensor_scalar(out=turns[:, 0], in0=turns[:, 1], scalar1=0.25, scalar2=None, op0=ALU.add)
-    whole_i = const.tile([P, 2, T, NF], I32)
+    whole_i = pool.tile([P, 2, T, NF], I32)
     nc.vector.tensor_copy(out=whole_i[:], in_=turns[:])
-    whole = const.tile([P, 2, T, NF], F32)
+    whole = pool.tile([P, 2, T, NF], F32)
     nc.vector.tensor_copy(out=whole[:], in_=whole_i[:])
-    frac = const.tile([P, 2, T, NF], F32)
+    frac = pool.tile([P, 2, T, NF], F32)
     nc.vector.tensor_tensor(out=frac[:], in0=turns[:], in1=whole[:], op=ALU.subtract)
-    neg = const.tile([P, 2, T, NF], F32)
+    rest = pool.tile([P, 2, T, NF], F32)
     flat = "p a t m -> p (a t m)"
     nc.vector.scalar_tensor_tensor(
-        out=neg[:].rearrange(flat),
+        out=rest[:].rearrange(flat),
         in0=frac[:].rearrange(flat),
         scalar=0.5,
         in1=frac[:].rearrange(flat),
         op0=ALU.is_gt,
         op1=ALU.subtract,
     )
+
     two_pi = 2.0 * math.pi
-    half = NF // 2
-
-    def sines():
-        sine_calls(nc, cos_t, sin_t, neg, two_pi, half)
-
-    return sines
-
-
-def sine_calls(nc, cos_t, sin_t, neg, two_pi, half):
     nc.scalar.activation(
         out=cos_t[:].rearrange("p t (m e) -> p t m e", e=2),
-        in_=neg[:, 0].unsqueeze(3).to_broadcast([P, T, NF, 2]),
+        in_=rest[:, 0].unsqueeze(3).to_broadcast([P, T, NF, 2]),
         func=ACT.Sin,
         scale=-two_pi,
     )
     for a in range(2):
         nc.scalar.activation(
-            out=sin_t[:, :, a * NF : (a + 1) * NF].rearrange("p t (m e) -> p t m e", e=2),
-            in_=neg[:, 1, :, a * half : (a + 1) * half].unsqueeze(3).to_broadcast([P, T, half, 2]),
+            out=sin_t[:, :, a * HALF : (a + 1) * HALF].rearrange("p t (m e) -> p t m e", e=2),
+            in_=rest[:, 1, :, a * HALF // 2 : (a + 1) * HALF // 2].unsqueeze(3).to_broadcast([P, T, HALF // 2, 2]),
             func=ACT.Sin,
             scale=two_pi if a == 0 else -two_pi,
         )
-
-
-N_UNITS = 24
-N_GROUPS = 6
-LOOKAHEAD = 12
-RAW_BUFS = 14
-ON_VECTOR = (1, 3, 12)
-ASSISTED = (5, 7, 9, 11, 14, 16, 18, 20, 22)
-HEAD_LOADS = ("u0", "u1", "x0", "u2", "x1", "u3", "x2", "u4", "x3", "u5", "u6", "u7", "u8", "u9", "u10", "u11")
 
 
 def tile_spikinggroupedslidingattention_pa_kernel(tc, x, Wq, Wk, Wv, out_0, out_1, out_2):
     nc = tc.nc
     with ExitStack() as ctx:
         const = ctx.enter_context(tc.tile_pool(name="const", bufs=1))
-        xpool = ctx.enter_context(tc.tile_pool(name="xpool", bufs=1))
         xgp = ctx.enter_context(tc.tile_pool(name="xgp", bufs=2))
         rawp = ctx.enter_context(tc.tile_pool(name="rawp", bufs=RAW_BUFS))
-        grpp = ctx.enter_context(tc.tile_pool(name="grpp", bufs=3))
+        grpp = ctx.enter_context(tc.tile_pool(name="grpp", bufs=4))
         wcp = ctx.enter_context(tc.tile_pool(name="wcp", bufs=3))
         prodp = ctx.enter_context(tc.tile_pool(name="prodp", bufs=3))
         outp = ctx.enter_context(tc.tile_pool(name="outp", bufs=3))
-        psum = ctx.enter_context(tc.psum_pool(name="psum", bufs=6))
-        psum_b = ctx.enter_context(tc.psum_pool(name="psum_b", bufs=2))
+        psum = ctx.enter_context(tc.psum_pool(name="psum", bufs=8))
 
         groups = [(Wk, 0, out_1, 0, True)]
-        for q in range(4):
-            groups.append((Wq, q * NCOL, out_0, q * HPG, True))
+        for quarter in range(4):
+            groups.append((Wq, quarter * NCOL, out_0, quarter * HPG, True))
         groups.append((Wv, 0, out_2, 0, False))
 
-        x_v = x.rearrange("b (p t) k -> p (b t) k", t=T)
-        x_sb = xpool.tile([P, T, D], BF16)
-        xc = xpool.tile([P, T, PASSES, P], U32, align_bytes=64)
-        xs = xpool.tile([P, T, PASSES, P], U8, align_bytes=64)
+        x_sb = const.tile([P, T, D], BF16)
+        x_codes = const.tile([P, T, PASSES, P], U32, align_bytes=64)
+        x_scales = const.tile([P, T, PASSES, P], U8, align_bytes=64)
         cos_t = const.tile([P, T, DH], F32)
         sin_t = const.tile([P, T, DH], F32)
         ident = const.tile([P, P], F32)
-        ident_b = const.tile([P, P], BF16)
 
         raw = {}
-        grp = {}
-        codes = {}
-        accs = {}
-        outs = {}
-        prods = {}
-        xts = {}
-        xgs = {}
+        grouped = {}
+        w_mx = {}
+        acc = {}
+        result = {}
+        x_t = {}
+        x_grouped = {}
+
+        def load_x(t):
+            nc.sync.dma_start(out=x_sb[:, t, :], in_=x.rearrange("b (p t) k -> p (b t) k", t=T)[:, t, :])
 
         def load_unit(u):
             w_dram, c0 = groups[u // PASSES][0:2]
@@ -150,177 +139,117 @@ def tile_spikinggroupedslidingattention_pa_kernel(tc, x, Wq, Wk, Wv, out_0, out_
                 in_=w_dram[g * K_PASS : (g + 1) * K_PASS, c0 : c0 + NCOL].rearrange("(p j) c -> p j c", j=PACK),
             )
 
-        def load_x(t):
-            nc.sync.dma_start(out=x_sb[:, t, :], in_=x_v[:, t, :])
-
-        def x_transposes(t):
+        def transpose_x(t):
             words = x_sb[:, t, :].bitcast(F32).rearrange("p (g q u) -> p g q u", g=PASSES, u=2)
-            for gp in range(PASSES // 2):
-                xt = psum.tile([P, 4, P], F32, tag="acc", name="xt")
-                xts[(t, gp)] = xt
-                for gl in range(2):
+            for half in range(2):
+                x_t[(t, half)] = psum.tile([P, 4, P], F32, tag="bank", name="x_t")
+                for g2 in range(2):
                     for u in range(2):
-                        nc.tensor.transpose(xt[:, 2 * gl + u, :], words[:, 2 * gp + gl, :, u], ident[:])
+                        nc.tensor.transpose(x_t[(t, half)][:, 2 * g2 + u, :], words[:, 2 * half + g2, :, u], ident[:])
 
-        def x_copies(t):
-            xgs[t] = xgp.tile([P, PASSES * P * PACK], BF16, align_bytes=64, name="xg")
-            xg_w = xgs[t][:].bitcast(F32).rearrange("p (g r u) -> p g r u", g=PASSES, u=2)
-            for gp in range(PASSES // 2):
-                src = xts[(t, gp)][:].rearrange("p (g u) r -> p g r u", u=2)
-                dst = xg_w[:, 2 * gp : 2 * gp + 2]
-                nc.scalar.copy(out=dst, in_=src)
+        def regroup_x(t):
+            x_grouped[t] = xgp.tile([P, PASSES * P * PACK], BF16, align_bytes=64, name="x_grouped")
+            dst = x_grouped[t][:].bitcast(F32).rearrange("p (g r u) -> p g r u", g=PASSES, u=2)
+            for half in range(2):
+                nc.scalar.copy(
+                    out=dst[:, 2 * half : 2 * half + 2], in_=x_t[(t, half)][:].rearrange("p (g u) r -> p g r u", u=2)
+                )
 
-        def x_quant(t):
+        def quantise_x(t):
             nc.vector.quantize_mx(
-                out=xc[:, t].rearrange("p g r -> p (g r)").bitcast(FP8X4),
-                scales=xs[:, t].rearrange("p g r -> p (g r)"),
-                in_=xgs[t][:],
+                out=x_codes[:, t].rearrange("p g r -> p (g r)").bitcast(FP8X4),
+                scales=x_scales[:, t].rearrange("p g r -> p (g r)"),
+                in_=x_grouped[t][:],
             )
 
-        def assist(u):
-            hc = NCOL // 2
-            for hh in range(2):
-                pb = psum_b.tile([P, hc, PACK], BF16, name="pb")
-                xts[("pb", u, hh)] = pb
-                for jp in range(PACK // 2):
-                    nc.tensor.matmul(
-                        out=pb[:, :, 2 * jp : 2 * jp + 2],
-                        lhsT=ident_b[:],
-                        rhs=raw[u][:, 2 * jp : 2 * jp + 2, hh * hc : (hh + 1) * hc].rearrange("p j c -> p c j"),
-                        start=True,
-                        stop=True,
-                    )
-
         def regroup(u):
-            grp[u] = grpp.tile([P, NCOL * PACK], BF16, align_bytes=64, name="grp")
-            if u in ASSISTED:
-                half = NCOL * PACK // 2
-                for hh in range(2):
-                    nc.scalar.copy(
-                        out=grp[u][:, hh * half : (hh + 1) * half],
-                        in_=xts[("pb", u, hh)][:].rearrange("p c j -> p (c j)"),
-                    )
-                return
-            dst = grp[u][:].rearrange("p (c i j) -> p c j i", i=4, j=PACK)
+            grouped[u] = grpp.tile([P, NCOL * PACK], BF16, align_bytes=64, name="grouped")
+            dst = grouped[u][:].rearrange("p (c i j) -> p c j i", i=4, j=PACK)
             src = raw[u][:].rearrange("p j (c i) -> p c j i", i=4)
-            if u in ON_VECTOR:
+            if groups[u // PASSES][4] and (u % PASSES == 1 or u == 3):
                 nc.vector.tensor_copy(out=dst, in_=src)
             else:
                 nc.scalar.copy(out=dst, in_=src)
 
-        def quant(u):
+        def quantise(u):
             n = u // PASSES
             g = u % PASSES
             if g == 0:
-                wc = wcp.tile([P, PASSES, NCOL], U32, align_bytes=64, name="wc")
-                ws = wcp.tile([P, PASSES, NCOL], U8, align_bytes=64, name="ws")
-                codes[n] = (wc, ws)
-            wc, ws = codes[n]
-            nc.vector.quantize_mx(out=wc[:, g, :].bitcast(FP8X4), scales=ws[:, g, :], in_=grp[u][:])
+                w_codes = wcp.tile([P, PASSES, NCOL], U32, align_bytes=64, name="w_codes")
+                w_scales = wcp.tile([P, PASSES, NCOL], U8, align_bytes=64, name="w_scales")
+                w_mx[n] = (w_codes, w_scales)
+            w_codes, w_scales = w_mx[n]
+            nc.vector.quantize_mx(out=w_codes[:, g, :].bitcast(FP8X4), scales=w_scales[:, g, :], in_=grouped[u][:])
 
-        def mx_pass(n, t, g):
-            wc, ws = codes[n]
+        def multiply(n, t, g):
+            if g == 0:
+                acc[(n, t)] = psum.tile([P, NCOL], F32, tag="bank", name="acc")
+            w_codes, w_scales = w_mx[n]
             nc.tensor.matmul_mx(
-                out=accs[(n, t)][:],
-                lhsT=xc[:, t, g, :].bitcast(FP8X4),
-                lhsT_scale=xs[:, t, g, :],
-                rhs=wc[:, g, :].bitcast(FP8X4),
-                rhs_scale=ws[:, g, :],
+                out=acc[(n, t)][:],
+                lhsT=x_codes[:, t, g, :].bitcast(FP8X4),
+                lhsT_scale=x_scales[:, t, g, :],
+                rhs=w_codes[:, g, :].bitcast(FP8X4),
+                rhs_scale=w_scales[:, g, :],
                 start=(g == 0),
                 stop=(g == PASSES - 1),
             )
 
-        def mx_tile(v):
-            n = v // T
-            t = v % T
-            accs[(n, t)] = psum.tile([P, NCOL], F32, tag="acc", name="acc")
-            for g in range(PASSES):
-                mx_pass(n, t, g)
-
-        def mx_unit(u):
-            n = u // PASSES
-            g = u % PASSES
-            for t in range(T):
-                if g == 0:
-                    accs[(n, t)] = psum.tile([P, NCOL], F32, tag="acc", name="acc")
-                mx_pass(n, t, g)
-
-        def rope(v):
-            n = v // T
-            t = v % T
+        def finish(n, t):
+            out_dram, h0, rotary = groups[n][2:5]
             if t == 0:
-                outs[n] = outp.tile([P, HPG, T, DH], F32, name="out_sb")
-            acc_h = accs[(n, t)][:].rearrange("p (h i) -> p h i", i=DH)
-            uq = prodp.tile([P, HPG, DH], F32, name="uq")
-            hw = DH // 2
-            for a in range(2):
+                result[n] = outp.tile([P, HPG, T, DH], F32, name="result")
+            res = result[n][:, :, t, :]
+            sums = acc[(n, t)][:].rearrange("p (h i) -> p h i", i=DH)
+            if rotary:
+                turned = prodp.tile([P, HPG, DH], F32, name="turned")
+                for a in range(2):
+                    nc.vector.tensor_tensor(
+                        out=turned[:, :, a * HALF : (a + 1) * HALF],
+                        in0=sums[:, :, (1 - a) * HALF : (2 - a) * HALF],
+                        in1=sin_t[:, t, a * HALF : (a + 1) * HALF].unsqueeze(1).to_broadcast([P, HPG, HALF]),
+                        op=ALU.mult,
+                    )
                 nc.vector.tensor_tensor(
-                    out=uq[:, :, a * hw : (a + 1) * hw],
-                    in0=acc_h[:, :, (1 - a) * hw : (2 - a) * hw],
-                    in1=sin_t[:, t, a * hw : (a + 1) * hw].unsqueeze(1).to_broadcast([P, HPG, hw]),
-                    op=ALU.mult,
+                    out=res, in0=sums, in1=cos_t[:, t, :].unsqueeze(1).to_broadcast([P, HPG, DH]), op=ALU.mult
                 )
-            nc.vector.tensor_tensor(
-                out=outs[n][:, :, t, :],
-                in0=acc_h,
-                in1=cos_t[:, t, :].unsqueeze(1).to_broadcast([P, HPG, DH]),
-                op=ALU.mult,
-            )
-            nc.gpsimd.tensor_tensor(out=outs[n][:, :, t, :], in0=outs[n][:, :, t, :], in1=uq[:], op=ALU.add)
-
-        def store(n):
-            out_dram, h0 = groups[n][2:4]
-            nc.sync.dma_start(
-                out=out_dram.rearrange("b h (p t) i -> p (b h) (t i)", t=T)[:, h0 : h0 + HPG, :],
-                in_=outs[n][:].rearrange("p h t i -> p h (t i)"),
-            )
-
-        def store_tile(n, t):
-            out_dram, h0 = groups[n][2:4]
-            nc.sync.dma_start(
-                out=out_dram.rearrange("b h (p t) i -> p t (b h) i", t=T)[:, t, h0 : h0 + HPG, :],
-                in_=outs[n][:, :, t, :],
-            )
-
-        for item in HEAD_LOADS:
-            if item[0] == "u":
-                load_unit(int(item[1:]))
+                nc.gpsimd.tensor_tensor(out=res, in0=res, in1=turned[:], op=ALU.add)
             else:
-                load_x(int(item[1:]))
-        tables = build_tables(nc, const, cos_t, sin_t)
-        masks.make_identity(nc, ident[:])
-        masks.make_identity(nc, ident_b[:])
+                nc.scalar.copy(out=res, in_=sums)
+            if n >= N_GROUPS - 2:
+                nc.sync.dma_start(
+                    out=out_dram.rearrange("b h (p t) i -> p t (b h) i", t=T)[:, t, h0 : h0 + HPG, :], in_=res
+                )
+            elif t == T - 1:
+                nc.sync.dma_start(
+                    out=out_dram.rearrange("b h (p t) i -> p (b h) (t i)", t=T)[:, h0 : h0 + HPG, :],
+                    in_=result[n][:].rearrange("p h t i -> p h (t i)"),
+                )
 
-        last = N_GROUPS - 1
-        for k in range(N_UNITS + 2):
-            if LOOKAHEAD <= k + LOOKAHEAD < N_UNITS:
+        for u in range(LOOKAHEAD):
+            load_unit(u)
+            if 1 <= u <= T:
+                load_x(u - 1)
+        rope_tables(nc, const, cos_t, sin_t)
+        masks.make_identity(nc, ident[:])
+
+        for k in range(N_UNITS + T + 1):
+            if k + LOOKAHEAD < N_UNITS:
                 load_unit(k + LOOKAHEAD)
-            if 0 <= k - 1 < T:
-                x_transposes(k - 1)
-            if k + 1 in ASSISTED:
-                assist(k + 1)
-            if 0 <= k - 1 < T:
-                x_copies(k - 1)
+            if 1 <= k <= T:
+                transpose_x(k - 1)
+                regroup_x(k - 1)
             if k < N_UNITS:
                 regroup(k)
-            if k == 1:
-                tables()
-            if 0 <= k - 1 < N_UNITS:
-                quant(k - 1)
-            if 0 <= k - 2 < T:
-                x_quant(k - 2)
-            if 0 <= k - 4 < last * T:
-                mx_tile(k - 4)
-            if last * PASSES <= k - 1 < N_UNITS:
-                mx_unit(k - 1)
-            if 0 <= k - 5 < last * T:
-                rope(k - 5)
-                if (k - 5) // T == last - 1:
-                    store_tile(last - 1, (k - 5) % T)
-                elif (k - 5) % T == T - 1:
-                    store((k - 5) // T)
-        outs[last] = outp.tile([P, HPG, T, DH], F32, name="out_sb")
-        for t in range(T):
-            acc_h = accs[(last, t)][:].rearrange("p (h i) -> p h i", i=DH)
-            nc.scalar.copy(out=outs[last][:, :, t, :], in_=acc_h)
-            store_tile(last, t)
+            if 1 <= k <= N_UNITS:
+                quantise(k - 1)
+            if 2 <= k <= T + 1:
+                quantise_x(k - 2)
+            if 1 <= k <= N_UNITS and (k - 1) // PASSES >= N_GROUPS - 2:
+                for t in range(T):
+                    multiply((k - 1) // PASSES, t, (k - 1) % PASSES)
+            if 4 <= k < 4 + (N_GROUPS - 2) * T:
+                for g in range(PASSES):
+                    multiply((k - 4) // T, (k - 4) % T, g)
+            if k >= T + 1:
+                finish((k - T - 1) // T, (k - T - 1) % T)

@@ -34,7 +34,7 @@ RAW_BUFS = LOOKAHEAD + 2
 FLOPS = 2 * S * D * (2048 + 512 + 512)
 
 
-def rope_tables(nc, pool, cos_t, sin_t):
+def rope_angles(nc, pool):
     warm = pool.tile([P, 2], F32)
     nc.vector.memset(warm[:, 0:1], 0.0)
     nc.scalar.activation(out=warm[:, 1:2], in_=warm[:, 0:1], func=ACT.Sin)
@@ -78,7 +78,10 @@ def rope_tables(nc, pool, cos_t, sin_t):
         op0=ALU.is_gt,
         op1=ALU.subtract,
     )
+    return rest
 
+
+def rope_tables(nc, rest, cos_t, sin_t):
     two_pi = 2.0 * math.pi
     nc.scalar.activation(
         out=cos_t[:].rearrange("p t (m e) -> p t m e", e=2),
@@ -99,9 +102,10 @@ def tile_spikinggroupedslidingattention_pa_kernel(tc, x, Wq, Wk, Wv, out_0, out_
     nc = tc.nc
     with ExitStack() as ctx:
         const = ctx.enter_context(tc.tile_pool(name="const", bufs=1))
+        xpool = ctx.enter_context(tc.tile_pool(name="xpool", bufs=1))
         xgp = ctx.enter_context(tc.tile_pool(name="xgp", bufs=2))
         rawp = ctx.enter_context(tc.tile_pool(name="rawp", bufs=RAW_BUFS))
-        grpp = ctx.enter_context(tc.tile_pool(name="grpp", bufs=4))
+        grpp = ctx.enter_context(tc.tile_pool(name="grpp", bufs=3))
         wcp = ctx.enter_context(tc.tile_pool(name="wcp", bufs=3))
         prodp = ctx.enter_context(tc.tile_pool(name="prodp", bufs=3))
         outp = ctx.enter_context(tc.tile_pool(name="outp", bufs=3))
@@ -112,9 +116,9 @@ def tile_spikinggroupedslidingattention_pa_kernel(tc, x, Wq, Wk, Wv, out_0, out_
             groups.append((Wq, quarter * NCOL, out_0, quarter * HPG, True))
         groups.append((Wv, 0, out_2, 0, False))
 
-        x_sb = const.tile([P, T, D], BF16)
-        x_codes = const.tile([P, T, PASSES, P], U32, align_bytes=64)
-        x_scales = const.tile([P, T, PASSES, P], U8, align_bytes=64)
+        x_sb = xpool.tile([P, T, D], BF16)
+        x_codes = xpool.tile([P, T, PASSES, P], U32, align_bytes=64)
+        x_scales = xpool.tile([P, T, PASSES, P], U8, align_bytes=64)
         cos_t = const.tile([P, T, DH], F32)
         sin_t = const.tile([P, T, DH], F32)
         ident = const.tile([P, P], F32)
@@ -166,7 +170,7 @@ def tile_spikinggroupedslidingattention_pa_kernel(tc, x, Wq, Wk, Wv, out_0, out_
             grouped[u] = grpp.tile([P, NCOL * PACK], BF16, align_bytes=64, name="grouped")
             dst = grouped[u][:].rearrange("p (c i j) -> p c j i", i=4, j=PACK)
             src = raw[u][:].rearrange("p j (c i) -> p c j i", i=4)
-            if groups[u // PASSES][4] and (u % PASSES == 1 or u == 3):
+            if u in (1, 3) or (u % PASSES == 0 and u >= 2 * PASSES):
                 nc.vector.tensor_copy(out=dst, in_=src)
             else:
                 nc.scalar.copy(out=dst, in_=src)
@@ -230,7 +234,7 @@ def tile_spikinggroupedslidingattention_pa_kernel(tc, x, Wq, Wk, Wv, out_0, out_
             load_unit(u)
             if 1 <= u <= T:
                 load_x(u - 1)
-        rope_tables(nc, const, cos_t, sin_t)
+        rest = rope_angles(nc, const)
         masks.make_identity(nc, ident[:])
 
         for k in range(N_UNITS + T + 1):
@@ -241,15 +245,17 @@ def tile_spikinggroupedslidingattention_pa_kernel(tc, x, Wq, Wk, Wv, out_0, out_
                 regroup_x(k - 1)
             if k < N_UNITS:
                 regroup(k)
+            if k == 1:
+                rope_tables(nc, rest, cos_t, sin_t)
             if 1 <= k <= N_UNITS:
                 quantise(k - 1)
             if 2 <= k <= T + 1:
                 quantise_x(k - 2)
-            if 1 <= k <= N_UNITS and (k - 1) // PASSES >= N_GROUPS - 2:
-                for t in range(T):
-                    multiply((k - 1) // PASSES, t, (k - 1) % PASSES)
-            if 4 <= k < 4 + (N_GROUPS - 2) * T:
+            if PASSES <= k < N_UNITS:
                 for g in range(PASSES):
-                    multiply((k - 4) // T, (k - 4) % T, g)
+                    multiply((k - PASSES) // T, (k - PASSES) % T, g)
+            if k > N_UNITS - PASSES and k <= N_UNITS:
+                for t in range(T):
+                    multiply(N_GROUPS - 1, t, (k - 1) % PASSES)
             if k >= T + 1:
                 finish((k - T - 1) // T, (k - T - 1) % T)

@@ -81,20 +81,20 @@ def rope_angles(nc, pool):
     return rest
 
 
-def rope_tables(nc, rest, cos_t, sin_t):
+def rope_tables(nc, rest, tab):
     two_pi = 2.0 * math.pi
     nc.scalar.activation(
-        out=cos_t[:].rearrange("p t (m e) -> p t m e", e=2),
-        in_=rest[:, 0].unsqueeze(3).to_broadcast([P, T, NF, 2]),
+        out=tab[:].rearrange("p t a w (m e) -> p (t a) w m e", e=2)[:, :, 0],
+        in_=rest[:, 0].rearrange("p t (a m) -> p (t a) m", a=2).unsqueeze(3).to_broadcast([P, T * 2, HALF // 2, 2]),
         func=ACT.Sin,
         scale=-two_pi,
     )
     for a in range(2):
         nc.scalar.activation(
-            out=sin_t[:, :, a * HALF : (a + 1) * HALF].rearrange("p t (m e) -> p t m e", e=2),
-            in_=rest[:, 1, :, a * HALF // 2 : (a + 1) * HALF // 2].unsqueeze(3).to_broadcast([P, T, HALF // 2, 2]),
+            out=tab[:, :, a, 1, :].rearrange("p t (m e) -> p t m e", e=2),
+            in_=rest[:, 1, :, (1 - a) * HALF // 2 : (2 - a) * HALF // 2].unsqueeze(3).to_broadcast([P, T, HALF // 2, 2]),
             func=ACT.Sin,
-            scale=two_pi if a == 0 else -two_pi,
+            scale=-two_pi if a == 0 else two_pi,
         )
 
 
@@ -119,8 +119,7 @@ def tile_spikinggroupedslidingattention_pa_kernel(tc, x, Wq, Wk, Wv, out_0, out_
         x_sb = xpool.tile([P, T, D], BF16)
         x_codes = xpool.tile([P, T, PASSES, P], U32, align_bytes=64)
         x_scales = xpool.tile([P, T, PASSES, P], U8, align_bytes=64)
-        cos_t = const.tile([P, T, DH], F32)
-        sin_t = const.tile([P, T, DH], F32)
+        tab = const.tile([P, T, 2, 2, HALF], F32)
         ident = const.tile([P, P], F32)
 
         raw = {}
@@ -206,18 +205,22 @@ def tile_spikinggroupedslidingattention_pa_kernel(tc, x, Wq, Wk, Wv, out_0, out_
             res = result[n][:, :, t, :]
             sums = acc[(n, t)][:].rearrange("p (h i) -> p h i", i=DH)
             if rotary:
-                turned = prodp.tile([P, HPG, DH], F32, name="turned")
-                for a in range(2):
-                    nc.vector.tensor_tensor(
-                        out=turned[:, :, a * HALF : (a + 1) * HALF],
-                        in0=sums[:, :, (1 - a) * HALF : (2 - a) * HALF],
-                        in1=sin_t[:, t, a * HALF : (a + 1) * HALF].unsqueeze(1).to_broadcast([P, HPG, HALF]),
-                        op=ALU.mult,
-                    )
+                prod = prodp.tile([P, HPG, 2, 2, HALF], F32, name="prod")
                 nc.vector.tensor_tensor(
-                    out=res, in0=sums, in1=cos_t[:, t, :].unsqueeze(1).to_broadcast([P, HPG, DH]), op=ALU.mult
+                    out=prod[:],
+                    in0=acc[(n, t)][:]
+                    .rearrange("p (h a i) -> p h a i", a=2, i=HALF)
+                    .unsqueeze(3)
+                    .to_broadcast([P, HPG, 2, 2, HALF]),
+                    in1=tab[:, t].unsqueeze(1).to_broadcast([P, HPG, 2, 2, HALF]),
+                    op=ALU.mult,
                 )
-                nc.gpsimd.tensor_tensor(out=res, in0=res, in1=turned[:], op=ALU.add)
+                nc.gpsimd.tensor_tensor(
+                    out=res.rearrange("p h (a i) -> p h a i", a=2),
+                    in0=prod[:, :, :, 0, :],
+                    in1=prod[:, :, ::-1, 1, :],
+                    op=ALU.add,
+                )
             else:
                 nc.scalar.copy(out=res, in_=sums)
             if n >= N_GROUPS - 2:
@@ -246,7 +249,7 @@ def tile_spikinggroupedslidingattention_pa_kernel(tc, x, Wq, Wk, Wv, out_0, out_
             if k < N_UNITS:
                 regroup(k)
             if k == 1:
-                rope_tables(nc, rest, cos_t, sin_t)
+                rope_tables(nc, rest, tab)
             if 1 <= k <= N_UNITS:
                 quantise(k - 1)
             if 2 <= k <= T + 1:

@@ -169,7 +169,7 @@ def tile_spikinggroupedslidingattention_pa_kernel(tc, x, Wq, Wk, Wv, out_0, out_
             grouped[u] = grpp.tile([P, NCOL * PACK], BF16, align_bytes=64, name="grouped")
             dst = grouped[u][:].rearrange("p (c i j) -> p c j i", i=4, j=PACK)
             src = raw[u][:].rearrange("p j (c i) -> p c j i", i=4)
-            if u in (1, 3) or (u % PASSES == 0 and u >= 2 * PASSES):
+            if u in (1, 3, 8, 12, 16):
                 nc.vector.tensor_copy(out=dst, in_=src)
             else:
                 nc.scalar.copy(out=dst, in_=src)
@@ -221,8 +221,10 @@ def tile_spikinggroupedslidingattention_pa_kernel(tc, x, Wq, Wk, Wv, out_0, out_
                     in1=prod[:, :, ::-1, 1, :],
                     op=ALU.add,
                 )
-            else:
+            elif t % 2 == 0:
                 nc.scalar.copy(out=res, in_=sums)
+            else:
+                nc.vector.tensor_copy(out=res, in_=sums)
             if n >= N_GROUPS - 2:
                 nc.sync.dma_start(
                     out=out_dram.rearrange("b h (p t) i -> p t (b h) i", t=T)[:, t, h0 : h0 + HPG, :], in_=res

@@ -167,8 +167,8 @@ def tile_spikinggroupedslidingattention_pa_kernel(tc, x, Wq, Wk, Wv, out_0, out_
 
         def regroup(u):
             grouped[u] = grpp.tile([P, NCOL * PACK], BF16, align_bytes=64, name="grouped")
-            dst = grouped[u][:].rearrange("p (c i j) -> p c j i", i=4, j=PACK)
-            src = raw[u][:].rearrange("p j (c i) -> p c j i", i=4)
+            dst = grouped[u][:].rearrange("p (c i j) -> p c j i", i=8, j=PACK)
+            src = raw[u][:].rearrange("p j (c i) -> p c j i", i=8)
             if u in (1, 3, 8, 12, 16):
                 nc.vector.tensor_copy(out=dst, in_=src)
             else:

@@ -215,7 +215,8 @@ def tile_spikinggroupedslidingattention_pa_kernel(tc, x, Wq, Wk, Wv, out_0, out_
                     in1=tab[:, t].unsqueeze(1).to_broadcast([P, HPG, 2, 2, HALF]),
                     op=ALU.mult,
                 )
-                nc.gpsimd.tensor_tensor(
+                adder = nc.vector if (n, t) == (N_GROUPS - 2, T - 1) else nc.gpsimd
+                adder.tensor_tensor(
                     out=res.rearrange("p h (a i) -> p h a i", a=2),
                     in0=prod[:, :, :, 0, :],
                     in1=prod[:, :, ::-1, 1, :],

@@ -28,8 +28,8 @@ NCOL = 512
 HPG = NCOL // DH
 N_GROUPS = 6
 N_UNITS = N_GROUPS * PASSES
-LOOKAHEAD = 12
-RAW_BUFS = LOOKAHEAD + 2
+RAW_BUFS = 14
+HEAD = 2 * T
 
 FLOPS = 2 * S * D * (2048 + 512 + 512)
 
@@ -105,9 +105,9 @@ def tile_spikinggroupedslidingattention_pa_kernel(tc, x, Wq, Wk, Wv, out_0, out_
         xpool = ctx.enter_context(tc.tile_pool(name="xpool", bufs=1))
         xgp = ctx.enter_context(tc.tile_pool(name="xgp", bufs=2))
         rawp = ctx.enter_context(tc.tile_pool(name="rawp", bufs=RAW_BUFS))
-        grpp = ctx.enter_context(tc.tile_pool(name="grpp", bufs=3))
+        grpp = ctx.enter_context(tc.tile_pool(name="grpp", bufs=6))
         wcp = ctx.enter_context(tc.tile_pool(name="wcp", bufs=3))
-        prodp = ctx.enter_context(tc.tile_pool(name="prodp", bufs=3))
+        prodp = ctx.enter_context(tc.tile_pool(name="prodp", bufs=4))
         outp = ctx.enter_context(tc.tile_pool(name="outp", bufs=3))
         psum = ctx.enter_context(tc.psum_pool(name="psum", bufs=8))
 
@@ -169,7 +169,7 @@ def tile_spikinggroupedslidingattention_pa_kernel(tc, x, Wq, Wk, Wv, out_0, out_
             grouped[u] = grpp.tile([P, NCOL * PACK], BF16, align_bytes=64, name="grouped")
             dst = grouped[u][:].rearrange("p (c i j) -> p c j i", i=8, j=PACK)
             src = raw[u][:].rearrange("p j (c i) -> p c j i", i=8)
-            if u in (1, 3, 8, 12, 16):
+            if u < HEAD and (u % 2 == 0 or u == HEAD - 1):
                 nc.vector.tensor_copy(out=dst, in_=src)
             else:
                 nc.scalar.copy(out=dst, in_=src)
@@ -236,32 +236,59 @@ def tile_spikinggroupedslidingattention_pa_kernel(tc, x, Wq, Wk, Wv, out_0, out_
                     in_=result[n][:].rearrange("p h t i -> p h (t i)"),
                 )
 
-        for u in range(LOOKAHEAD):
+        def multiply_group(n):
+            for t in range(T):
+                for g in range(PASSES):
+                    multiply(n, t, g)
+
+        def quantise_and_multiply(u):
+            quantise(u)
+            n = u // PASSES
+            if n == N_GROUPS - 1:
+                for t in range(T):
+                    multiply(n, t, u % PASSES)
+            elif u % PASSES == PASSES - 1:
+                multiply_group(n)
+
+        for t in range(T):
+            load_x(t)
+            load_unit(2 * t)
+            load_unit(2 * t + 1)
+        for u in range(HEAD, RAW_BUFS):
             load_unit(u)
-            if 1 <= u <= T:
-                load_x(u - 1)
         rest = rope_angles(nc, const)
         masks.make_identity(nc, ident[:])
 
-        for k in range(N_UNITS + T + 1):
-            if k + LOOKAHEAD < N_UNITS:
-                load_unit(k + LOOKAHEAD)
-            if 1 <= k <= T:
-                transpose_x(k - 1)
-                regroup_x(k - 1)
-            if k < N_UNITS:
-                regroup(k)
-            if k == 1:
-                rope_tables(nc, rest, tab)
-            if 1 <= k <= N_UNITS:
-                quantise(k - 1)
-            if 2 <= k <= T + 1:
-                quantise_x(k - 2)
-            if PASSES <= k < N_UNITS:
-                for g in range(PASSES):
-                    multiply((k - PASSES) // T, (k - PASSES) % T, g)
-            if k > N_UNITS - PASSES and k <= N_UNITS:
-                for t in range(T):
-                    multiply(N_GROUPS - 1, t, (k - 1) % PASSES)
-            if k >= T + 1:
-                finish((k - T - 1) // T, (k - T - 1) % T)
+        ctx.enter_context(tc.manual_schedule())
+        rope_tables(nc, rest, tab)
+        for t in range(T):
+            transpose_x(t)
+            regroup_x(t)
+            regroup(2 * t)
+            regroup(2 * t + 1)
+            load_unit(RAW_BUFS + 2 * t)
+            load_unit(RAW_BUFS + 2 * t + 1)
+            quantise_x(t)
+            if t > 0:
+                quantise(2 * t - 1)
+            quantise(2 * t)
+        quantise(HEAD - 1)
+        for n in range(HEAD // PASSES):
+            multiply_group(n)
+
+        tiles = [(n, t) for n in range(N_GROUPS) for t in range(T)]
+        done = 3
+        for n, t in tiles[:done]:
+            finish(n, t)
+        for u in range(HEAD, N_UNITS):
+            regroup(u)
+            if u + RAW_BUFS < N_UNITS:
+                load_unit(u + RAW_BUFS)
+            if u > HEAD:
+                quantise_and_multiply(u - 1)
+                finish(*tiles[done])
+                done += 1
+        finish(*tiles[done])
+        quantise_and_multiply(N_UNITS - 1)
+        for n, t in tiles[done + 1 :]:
+            finish(n, t)

@@ -29,7 +29,7 @@ HPG = NCOL // DH
 N_GROUPS = 6
 N_UNITS = N_GROUPS * PASSES
 RAW_BUFS = 14
-HEAD = 2 * T
+HEAD = 12
 
 FLOPS = 2 * S * D * (2048 + 512 + 512)
 
@@ -39,35 +39,46 @@ def rope_angles(nc, pool):
     nc.vector.memset(warm[:, 0:1], 0.0)
     nc.scalar.activation(out=warm[:, 1:2], in_=warm[:, 0:1], func=ACT.Sin)
 
-    freq = pool.tile([P, NF], F32)
-    nc.vector.memset(freq[:, 0:1], 1.0)
+    side = 8
+    rows = pool.tile([P, 2, side], F32)
+    nc.vector.memset(rows[:, :, 0:1], 1.0)
     nc.vector.tensor_scalar(
-        out=freq[:, 0:1], in0=freq[:, 0:1], scalar1=1.0 / (2.0 * math.pi), scalar2=None, op0=ALU.mult
+        out=rows[:, 0, 0:1], in0=rows[:, 0, 0:1], scalar1=1.0 / (2.0 * math.pi), scalar2=None, op0=ALU.mult
     )
-    ratio = THETA ** (-1.0 / NF)
     w = 1
-    while w < NF:
-        nc.vector.tensor_scalar(
-            out=freq[:, w : 2 * w], in0=freq[:, 0:w], scalar1=ratio**w, scalar2=None, op0=ALU.mult
-        )
+    while w < side:
+        for r, step in ((1, 1), (0, side)):
+            nc.vector.tensor_scalar(
+                out=rows[:, r, w : 2 * w],
+                in0=rows[:, r, 0:w],
+                scalar1=THETA ** (-w * step / NF),
+                scalar2=None,
+                op0=ALU.mult,
+            )
         w = 2 * w
-
-    pos_i = pool.tile([P, T, NF], I32)
-    nc.gpsimd.iota(pos_i[:], pattern=[[1, T], [0, NF]], base=0, channel_multiplier=T)
-    pos = pool.tile([P, T, NF], F32)
-    nc.vector.tensor_copy(out=pos[:], in_=pos_i[:])
-
-    turns = pool.tile([P, 2, T, NF], F32)
+    freq = pool.tile([P, side, side], F32)
     nc.vector.tensor_tensor(
-        out=turns[:, 1], in0=pos[:], in1=freq[:].unsqueeze(1).to_broadcast([P, T, NF]), op=ALU.mult
+        out=freq[:],
+        in0=rows[:, 0].unsqueeze(2).to_broadcast([P, side, side]),
+        in1=rows[:, 1].unsqueeze(1).to_broadcast([P, side, side]),
+        op=ALU.mult,
     )
-    nc.vector.tensor_scalar(out=turns[:, 0], in0=turns[:, 1], scalar1=0.25, scalar2=None, op0=ALU.add)
-    whole_i = pool.tile([P, 2, T, NF], I32)
-    nc.vector.tensor_copy(out=whole_i[:], in_=turns[:])
-    whole = pool.tile([P, 2, T, NF], F32)
-    nc.vector.tensor_copy(out=whole[:], in_=whole_i[:])
+
+    pos = pool.tile([P, T], I32)
+    nc.gpsimd.iota(pos[:], pattern=[[1, T]], base=0, channel_multiplier=T)
+
+    turns = pool.tile([P, T, NF], F32)
+    nc.vector.tensor_tensor(
+        out=turns[:],
+        in0=freq[:].rearrange("p a b -> p (a b)").unsqueeze(1).to_broadcast([P, T, NF]),
+        in1=pos[:].unsqueeze(2).to_broadcast([P, T, NF]),
+        op=ALU.mult,
+    )
+    whole = pool.tile([P, T, NF], I32)
+    nc.vector.tensor_copy(out=whole[:], in_=turns[:])
     frac = pool.tile([P, 2, T, NF], F32)
-    nc.vector.tensor_tensor(out=frac[:], in0=turns[:], in1=whole[:], op=ALU.subtract)
+    nc.vector.tensor_tensor(out=frac[:, 1], in0=turns[:], in1=whole[:], op=ALU.subtract)
+    nc.vector.tensor_scalar(out=frac[:, 0], in0=frac[:, 1], scalar1=0.25, scalar2=None, op0=ALU.add)
     rest = pool.tile([P, 2, T, NF], F32)
     flat = "p a t m -> p (a t m)"
     nc.vector.scalar_tensor_tensor(
@@ -105,7 +116,7 @@ def tile_spikinggroupedslidingattention_pa_kernel(tc, x, Wq, Wk, Wv, out_0, out_
         xpool = ctx.enter_context(tc.tile_pool(name="xpool", bufs=1))
         xgp = ctx.enter_context(tc.tile_pool(name="xgp", bufs=2))
         rawp = ctx.enter_context(tc.tile_pool(name="rawp", bufs=RAW_BUFS))
-        grpp = ctx.enter_context(tc.tile_pool(name="grpp", bufs=6))
+        grpp = ctx.enter_context(tc.tile_pool(name="grpp", bufs=8))
         wcp = ctx.enter_context(tc.tile_pool(name="wcp", bufs=3))
         prodp = ctx.enter_context(tc.tile_pool(name="prodp", bufs=4))
         outp = ctx.enter_context(tc.tile_pool(name="outp", bufs=3))
@@ -169,7 +180,7 @@ def tile_spikinggroupedslidingattention_pa_kernel(tc, x, Wq, Wk, Wv, out_0, out_
             grouped[u] = grpp.tile([P, NCOL * PACK], BF16, align_bytes=64, name="grouped")
             dst = grouped[u][:].rearrange("p (c i j) -> p c j i", i=8, j=PACK)
             src = raw[u][:].rearrange("p j (c i) -> p c j i", i=8)
-            if u < HEAD and (u % 2 == 0 or u == HEAD - 1):
+            if u == 0 or (u < HEAD and u % 2 == 1):
                 nc.vector.tensor_copy(out=dst, in_=src)
             else:
                 nc.scalar.copy(out=dst, in_=src)
@@ -236,10 +247,13 @@ def tile_spikinggroupedslidingattention_pa_kernel(tc, x, Wq, Wk, Wv, out_0, out_
                     in_=result[n][:].rearrange("p h t i -> p h (t i)"),
                 )
 
+        def multiply_tile(n, t):
+            for g in range(PASSES):
+                multiply(n, t, g)
+
         def multiply_group(n):
             for t in range(T):
-                for g in range(PASSES):
-                    multiply(n, t, g)
+                multiply_tile(n, t)
 
         def quantise_and_multiply(u):
             quantise(u)
@@ -250,45 +264,50 @@ def tile_spikinggroupedslidingattention_pa_kernel(tc, x, Wq, Wk, Wv, out_0, out_
             elif u % PASSES == PASSES - 1:
                 multiply_group(n)
 
-        for t in range(T):
-            load_x(t)
-            load_unit(2 * t)
-            load_unit(2 * t + 1)
-        for u in range(HEAD, RAW_BUFS):
+        x_step = {0: 0, 1: 1, 3: 2, 4: 3}
+        load_x(0)
+        for u in range(RAW_BUFS):
+            if u > 1 and u % 2 == 1 and u // 2 in x_step:
+                load_x(x_step[u // 2])
             load_unit(u)
         rest = rope_angles(nc, const)
         masks.make_identity(nc, ident[:])
 
-        ctx.enter_context(tc.manual_schedule())
-        rope_tables(nc, rest, tab)
-        for t in range(T):
-            transpose_x(t)
-            regroup_x(t)
-            regroup(2 * t)
-            regroup(2 * t + 1)
-            load_unit(RAW_BUFS + 2 * t)
-            load_unit(RAW_BUFS + 2 * t + 1)
-            quantise_x(t)
-            if t > 0:
-                quantise(2 * t - 1)
-            quantise(2 * t)
-        quantise(HEAD - 1)
-        for n in range(HEAD // PASSES):
-            multiply_group(n)
-
-        tiles = [(n, t) for n in range(N_GROUPS) for t in range(T)]
-        done = 3
-        for n, t in tiles[:done]:
-            finish(n, t)
-        for u in range(HEAD, N_UNITS):
+        def regroup_and_load(u):
             regroup(u)
             if u + RAW_BUFS < N_UNITS:
                 load_unit(u + RAW_BUFS)
-            if u > HEAD:
-                quantise_and_multiply(u - 1)
-                finish(*tiles[done])
-                done += 1
-        finish(*tiles[done])
-        quantise_and_multiply(N_UNITS - 1)
-        for n, t in tiles[done + 1 :]:
+
+        tiles = [(n, t) for n in range(N_GROUPS) for t in range(T)]
+        ctx.enter_context(tc.manual_schedule())
+        for i in range(HEAD // 2):
+            if i in x_step:
+                transpose_x(x_step[i])
+                regroup_x(x_step[i])
+            if i == 0:
+                regroup_and_load(0)
+                rope_tables(nc, rest, tab)
+            regroup_and_load(2 * i + 1)
+            regroup_and_load(2 * i + 2)
+            if i == 2:
+                finish(*tiles[0])
+            quantise(2 * i)
+            quantise(2 * i + 1)
+            if i in x_step:
+                quantise_x(x_step[i])
+            if i == 1:
+                for t in range(2):
+                    multiply_tile(0, t)
+            if i == 4:
+                for n, t in tiles[2 : 2 * T]:
+                    multiply_tile(n, t)
+        multiply_group(2)
+        for n, t in tiles[1:8]:
             finish(n, t)
+        for u in range(HEAD, N_UNITS):
+            if u > HEAD:
+                regroup_and_load(u)
+            quantise_and_multiply(u)
+            finish(*tiles[u - HEAD + 8])
+        for t in range(T):
+            finish(N_GROUPS - 1, t)

@@ -270,7 +270,6 @@ def tile_spikinggroupedslidingattention_pa_kernel(tc, x, Wq, Wk, Wv, out_0, out_
             if u > 1 and u % 2 == 1 and u // 2 in x_step:
                 load_x(x_step[u // 2])
             load_unit(u)
-        rest = rope_angles(nc, const)
         masks.make_identity(nc, ident[:])
 
         def regroup_and_load(u):
@@ -280,6 +279,7 @@ def tile_spikinggroupedslidingattention_pa_kernel(tc, x, Wq, Wk, Wv, out_0, out_
 
         tiles = [(n, t) for n in range(N_GROUPS) for t in range(T)]
         ctx.enter_context(tc.manual_schedule())
+        rest = rope_angles(nc, const)
         for i in range(HEAD // 2):
             if i in x_step:
                 transpose_x(x_step[i])

@@ -29,7 +29,7 @@ HPG = NCOL // DH
 N_GROUPS = 6
 N_UNITS = N_GROUPS * PASSES
 RAW_BUFS = 14
-HEAD = 12
+VECTOR_UNITS = (1, 2, 3, 5, 7, 8, 10)
 
 FLOPS = 2 * S * D * (2048 + 512 + 512)
 
@@ -116,9 +116,9 @@ def tile_spikinggroupedslidingattention_pa_kernel(tc, x, Wq, Wk, Wv, out_0, out_
         xpool = ctx.enter_context(tc.tile_pool(name="xpool", bufs=1))
         xgp = ctx.enter_context(tc.tile_pool(name="xgp", bufs=2))
         rawp = ctx.enter_context(tc.tile_pool(name="rawp", bufs=RAW_BUFS))
-        grpp = ctx.enter_context(tc.tile_pool(name="grpp", bufs=8))
+        grpp = ctx.enter_context(tc.tile_pool(name="grpp", bufs=4))
         wcp = ctx.enter_context(tc.tile_pool(name="wcp", bufs=3))
-        prodp = ctx.enter_context(tc.tile_pool(name="prodp", bufs=4))
+        prodp = ctx.enter_context(tc.tile_pool(name="prodp", bufs=3))
         outp = ctx.enter_context(tc.tile_pool(name="outp", bufs=3))
         psum = ctx.enter_context(tc.psum_pool(name="psum", bufs=8))
 
@@ -137,6 +137,7 @@ def tile_spikinggroupedslidingattention_pa_kernel(tc, x, Wq, Wk, Wv, out_0, out_
         grouped = {}
         w_mx = {}
         acc = {}
+        prod = {}
         result = {}
         x_t = {}
         x_grouped = {}
@@ -177,15 +178,18 @@ def tile_spikinggroupedslidingattention_pa_kernel(tc, x, Wq, Wk, Wv, out_0, out_
             )
 
         def regroup(u):
-            grouped[u] = grpp.tile([P, NCOL * PACK], BF16, align_bytes=64, name="grouped")
-            dst = grouped[u][:].rearrange("p (c i j) -> p c j i", i=8, j=PACK)
+            if u // 2 not in grouped:
+                grouped[u // 2] = grpp.tile([P, 2, NCOL * PACK], BF16, align_bytes=64, name="grouped")
+            dst = grouped[u // 2][:, u % 2, :].rearrange("p (c i j) -> p c j i", i=8, j=PACK)
             src = raw[u][:].rearrange("p j (c i) -> p c j i", i=8)
-            if u == 0 or (u < HEAD and u % 2 == 1):
+            if u in VECTOR_UNITS:
                 nc.vector.tensor_copy(out=dst, in_=src)
             else:
                 nc.scalar.copy(out=dst, in_=src)
+            if u + RAW_BUFS < N_UNITS:
+                load_unit(u + RAW_BUFS)
 
-        def quantise(u):
+        def quantise(u, count=1):
             n = u // PASSES
             g = u % PASSES
             if g == 0:
@@ -193,7 +197,11 @@ def tile_spikinggroupedslidingattention_pa_kernel(tc, x, Wq, Wk, Wv, out_0, out_
                 w_scales = wcp.tile([P, PASSES, NCOL], U8, align_bytes=64, name="w_scales")
                 w_mx[n] = (w_codes, w_scales)
             w_codes, w_scales = w_mx[n]
-            nc.vector.quantize_mx(out=w_codes[:, g, :].bitcast(FP8X4), scales=w_scales[:, g, :], in_=grouped[u][:])
+            nc.vector.quantize_mx(
+                out=w_codes[:, g : g + count, :].rearrange("p g c -> p (g c)").bitcast(FP8X4),
+                scales=w_scales[:, g : g + count, :].rearrange("p g c -> p (g c)"),
+                in_=grouped[u // 2][:, u % 2 : u % 2 + count, :].rearrange("p e c -> p (e c)"),
+            )
 
         def multiply(n, t, g):
             if g == 0:
@@ -209,43 +217,47 @@ def tile_spikinggroupedslidingattention_pa_kernel(tc, x, Wq, Wk, Wv, out_0, out_
                 stop=(g == PASSES - 1),
             )
 
-        def finish(n, t):
-            out_dram, h0, rotary = groups[n][2:5]
+        def products(n, t):
             if t == 0:
                 result[n] = outp.tile([P, HPG, T, DH], F32, name="result")
-            res = result[n][:, :, t, :]
-            sums = acc[(n, t)][:].rearrange("p (h i) -> p h i", i=DH)
-            if rotary:
-                prod = prodp.tile([P, HPG, 2, 2, HALF], F32, name="prod")
-                nc.vector.tensor_tensor(
-                    out=prod[:],
-                    in0=acc[(n, t)][:]
-                    .rearrange("p (h a i) -> p h a i", a=2, i=HALF)
-                    .unsqueeze(3)
-                    .to_broadcast([P, HPG, 2, 2, HALF]),
-                    in1=tab[:, t].unsqueeze(1).to_broadcast([P, HPG, 2, 2, HALF]),
-                    op=ALU.mult,
-                )
-                adder = nc.vector if (n, t) == (N_GROUPS - 2, T - 1) else nc.gpsimd
-                adder.tensor_tensor(
-                    out=res.rearrange("p h (a i) -> p h a i", a=2),
-                    in0=prod[:, :, :, 0, :],
-                    in1=prod[:, :, ::-1, 1, :],
-                    op=ALU.add,
-                )
-            elif t % 2 == 0:
-                nc.scalar.copy(out=res, in_=sums)
-            else:
-                nc.vector.tensor_copy(out=res, in_=sums)
-            if n >= N_GROUPS - 2:
-                nc.sync.dma_start(
-                    out=out_dram.rearrange("b h (p t) i -> p t (b h) i", t=T)[:, t, h0 : h0 + HPG, :], in_=res
-                )
-            elif t == T - 1:
-                nc.sync.dma_start(
-                    out=out_dram.rearrange("b h (p t) i -> p (b h) (t i)", t=T)[:, h0 : h0 + HPG, :],
-                    in_=result[n][:].rearrange("p h t i -> p h (t i)"),
-                )
+            if t % 2 == 0:
+                prod[(n, t // 2)] = prodp.tile([P, HPG, 2, 2, 2, HALF], F32, name="pair")
+            nc.vector.tensor_tensor(
+                out=prod[(n, t // 2)][:, :, t % 2],
+                in0=acc[(n, t)][:]
+                .rearrange("p (h a i) -> p h a i", a=2, i=HALF)
+                .unsqueeze(3)
+                .to_broadcast([P, HPG, 2, 2, HALF]),
+                in1=tab[:, t].unsqueeze(1).to_broadcast([P, HPG, 2, 2, HALF]),
+                op=ALU.mult,
+            )
+
+        def add(engine, n, t, count):
+            both = prod[(n, t // 2)][:, :, t % 2 : t % 2 + count]
+            engine.tensor_tensor(
+                out=result[n][:, :, t : t + count, :].rearrange("p h t (a i) -> p h t a i", a=2),
+                in0=both[:, :, :, :, 0, :],
+                in1=both[:, :, :, ::-1, 1, :],
+                op=ALU.add,
+            )
+
+        def store(n, t, count):
+            out_dram, h0 = groups[n][2:4]
+            nc.sync.dma_start(
+                out=out_dram.rearrange("b h (p t) i -> p (b h) t i", t=T)[:, h0 : h0 + HPG, t : t + count, :],
+                in_=result[n][:, :, t : t + count, :],
+            )
+
+        def rotate_pair(pair):
+            n = pair // 2
+            t = 2 * (pair % 2)
+            products(n, t)
+            products(n, t + 1)
+            add(nc.gpsimd, n, t, 2)
+            if n == N_GROUPS - 2:
+                store(n, t, 2)
+            elif t > 0:
+                store(n, 0, T)
 
         def multiply_tile(n, t):
             for g in range(PASSES):
@@ -255,59 +267,94 @@ def tile_spikinggroupedslidingattention_pa_kernel(tc, x, Wq, Wk, Wv, out_0, out_
             for t in range(T):
                 multiply_tile(n, t)
 
-        def quantise_and_multiply(u):
-            quantise(u)
-            n = u // PASSES
-            if n == N_GROUPS - 1:
-                for t in range(T):
-                    multiply(n, t, u % PASSES)
-            elif u % PASSES == PASSES - 1:
-                multiply_group(n)
+        def empty(n, t, engine_copy):
+            if t == 0:
+                result[n] = outp.tile([P, HPG, T, DH], F32, name="result")
+            engine_copy(out=result[n][:, :, t, :], in_=acc[(n, t)][:].rearrange("p (h i) -> p h i", i=DH))
+            store(n, t, 1)
 
-        x_step = {0: 0, 1: 1, 3: 2, 4: 3}
-        load_x(0)
-        for u in range(RAW_BUFS):
-            if u > 1 and u % 2 == 1 and u // 2 in x_step:
-                load_x(x_step[u // 2])
+        def bring_x(t):
+            transpose_x(t)
+            regroup_x(t)
+
+        for first, x_tiles in ((0, (0,)), (3, (1,)), (6, (2, 3))):
+            for u in range(first, first + 3):
+                if u < 8:
+                    load_unit(u)
+            for t in x_tiles:
+                load_x(t)
+        for u in range(8, RAW_BUFS):
             load_unit(u)
         masks.make_identity(nc, ident[:])
 
-        def regroup_and_load(u):
-            regroup(u)
-            if u + RAW_BUFS < N_UNITS:
-                load_unit(u + RAW_BUFS)
-
-        tiles = [(n, t) for n in range(N_GROUPS) for t in range(T)]
         ctx.enter_context(tc.manual_schedule())
         rest = rope_angles(nc, const)
-        for i in range(HEAD // 2):
-            if i in x_step:
-                transpose_x(x_step[i])
-                regroup_x(x_step[i])
-            if i == 0:
-                regroup_and_load(0)
-                rope_tables(nc, rest, tab)
-            regroup_and_load(2 * i + 1)
-            regroup_and_load(2 * i + 2)
-            if i == 2:
-                finish(*tiles[0])
-            quantise(2 * i)
-            quantise(2 * i + 1)
-            if i in x_step:
-                quantise_x(x_step[i])
-            if i == 1:
-                for t in range(2):
-                    multiply_tile(0, t)
-            if i == 4:
-                for n, t in tiles[2 : 2 * T]:
-                    multiply_tile(n, t)
-        multiply_group(2)
-        for n, t in tiles[1:8]:
-            finish(n, t)
-        for u in range(HEAD, N_UNITS):
-            if u > HEAD:
-                regroup_and_load(u)
-            quantise_and_multiply(u)
-            finish(*tiles[u - HEAD + 8])
+        regroup(0)
+        rope_tables(nc, rest, tab)
+        regroup(1)
+        regroup(2)
+        quantise(0)
+        quantise(1)
+        quantise(2)
+        regroup(3)
+        quantise(3)
+        regroup(4)
+        bring_x(0)
+        regroup(5)
+        quantise(4)
+        quantise(5)
+        quantise_x(0)
+        regroup(6)
+        bring_x(1)
+        regroup(7)
+        quantise(6)
+        quantise(7)
+        quantise_x(1)
+        bring_x(2)
+        bring_x(3)
+        multiply_tile(0, 0)
+        multiply_tile(0, 1)
+        regroup(8)
+        quantise_x(2)
+        quantise(8)
+        rotate_pair(0)
+        regroup(9)
+        regroup(10)
+        quantise_x(3)
+        multiply_tile(0, 2)
+        multiply_tile(0, 3)
+        multiply_group(1)
+        rotate_pair(1)
+        quantise(9)
+        rotate_pair(2)
+        for u in range(10, N_UNITS - 2, 2):
+            if u > 10:
+                regroup(u)
+            regroup(u + 1)
+            quantise(u, 2)
+            n = u // PASSES
+            if n == N_GROUPS - 1:
+                for g in range(2):
+                    for t in range(T):
+                        multiply(n, t, g)
+            elif u % PASSES == 2:
+                multiply_group(n)
+            rotate_pair(u // 2 - 2)
+        n = N_GROUPS - 2
+        regroup(N_UNITS - 2)
+        regroup(N_UNITS - 1)
+        quantise(N_UNITS - 2)
         for t in range(T):
-            finish(N_GROUPS - 1, t)
+            multiply(n + 1, t, 2)
+        products(n, 2)
+        quantise(N_UNITS - 1)
+        for t in range(T):
+            multiply(n + 1, t, 3)
+        add(nc.vector, n, 2, 1)
+        store(n, 2, 1)
+        products(n, 3)
+        for t in range(T - 1):
+            empty(n + 1, t, nc.scalar.copy)
+        empty(n + 1, T - 1, nc.vector.tensor_copy)
+        add(nc.vector, n, 3, 1)
+        store(n, 3, 1)

@@ -29,7 +29,7 @@ HPG = NCOL // DH
 N_GROUPS = 6
 N_UNITS = N_GROUPS * PASSES
 RAW_BUFS = 14
-VECTOR_UNITS = (1, 2, 3, 5, 7, 8, 10)
+VECTOR_UNITS = (0, 1, 3, 5, 7, 8, 10)
 
 FLOPS = 2 * S * D * (2048 + 512 + 512)
 
@@ -40,45 +40,52 @@ def rope_angles(nc, pool):
     nc.scalar.activation(out=warm[:, 1:2], in_=warm[:, 0:1], func=ACT.Sin)
 
     side = 8
+    half = side // 2
+    one = pool.tile([P, 1], F32)
+    nc.vector.memset(one[:], 1.0)
     rows = pool.tile([P, 2, side], F32)
-    nc.vector.memset(rows[:, :, 0:1], 1.0)
-    nc.vector.tensor_scalar(
-        out=rows[:, 0, 0:1], in0=rows[:, 0, 0:1], scalar1=1.0 / (2.0 * math.pi), scalar2=None, op0=ALU.mult
-    )
-    w = 1
-    while w < side:
-        for r, step in ((1, 1), (0, side)):
+    for r, step, first in ((0, side, 1.0 / (2.0 * math.pi)), (1, 1, 1.0)):
+        for c in range(half):
             nc.vector.tensor_scalar(
-                out=rows[:, r, w : 2 * w],
-                in0=rows[:, r, 0:w],
-                scalar1=THETA ** (-w * step / NF),
+                out=rows[:, r, c : c + 1],
+                in0=one[:],
+                scalar1=first * THETA ** (-c * step / NF),
                 scalar2=None,
                 op0=ALU.mult,
             )
-        w = 2 * w
-    freq = pool.tile([P, side, side], F32)
-    nc.vector.tensor_tensor(
-        out=freq[:],
-        in0=rows[:, 0].unsqueeze(2).to_broadcast([P, side, side]),
-        in1=rows[:, 1].unsqueeze(1).to_broadcast([P, side, side]),
-        op=ALU.mult,
-    )
+    for r, step in ((0, side), (1, 1)):
+        nc.vector.tensor_scalar(
+            out=rows[:, r, half:],
+            in0=rows[:, r, :half],
+            scalar1=THETA ** (-half * step / NF),
+            scalar2=None,
+            op0=ALU.mult,
+        )
 
     pos = pool.tile([P, T], I32)
     nc.gpsimd.iota(pos[:], pattern=[[1, T]], base=0, channel_multiplier=T)
 
+    coarse = pool.tile([P, T, side], F32)
+    nc.vector.tensor_tensor(
+        out=coarse[:],
+        in0=rows[:, 0].unsqueeze(1).to_broadcast([P, T, side]),
+        in1=pos[:].unsqueeze(2).to_broadcast([P, T, side]),
+        op=ALU.mult,
+    )
     turns = pool.tile([P, T, NF], F32)
     nc.vector.tensor_tensor(
-        out=turns[:],
-        in0=freq[:].rearrange("p a b -> p (a b)").unsqueeze(1).to_broadcast([P, T, NF]),
-        in1=pos[:].unsqueeze(2).to_broadcast([P, T, NF]),
+        out=turns[:].rearrange("p t (a b) -> p t a b", a=side),
+        in0=coarse[:].unsqueeze(3).to_broadcast([P, T, side, side]),
+        in1=rows[:, 1].unsqueeze(1).unsqueeze(1).to_broadcast([P, T, side, side]),
         op=ALU.mult,
     )
     whole = pool.tile([P, T, NF], I32)
     nc.vector.tensor_copy(out=whole[:], in_=turns[:])
     frac = pool.tile([P, 2, T, NF], F32)
     nc.vector.tensor_tensor(out=frac[:, 1], in0=turns[:], in1=whole[:], op=ALU.subtract)
-    nc.vector.tensor_scalar(out=frac[:, 0], in0=frac[:, 1], scalar1=0.25, scalar2=None, op0=ALU.add)
+    nc.vector.scalar_tensor_tensor(
+        out=frac[:, 0], in0=turns[:], scalar=0.25, in1=whole[:], op0=ALU.add, op1=ALU.subtract
+    )
     rest = pool.tile([P, 2, T, NF], F32)
     flat = "p a t m -> p (a t m)"
     nc.vector.scalar_tensor_tensor(
@@ -94,16 +101,17 @@ def rope_angles(nc, pool):
 
 def rope_tables(nc, rest, tab):
     two_pi = 2.0 * math.pi
+    quarter = NF // 2
     nc.scalar.activation(
-        out=tab[:].rearrange("p t a w (m e) -> p (t a) w m e", e=2)[:, :, 0],
-        in_=rest[:, 0].rearrange("p t (a m) -> p (t a) m", a=2).unsqueeze(3).to_broadcast([P, T * 2, HALF // 2, 2]),
+        out=tab[:, :, :, 0, :],
+        in_=rest[:, 0].rearrange("p t (a m) -> p t a m", a=2),
         func=ACT.Sin,
         scale=-two_pi,
     )
     for a in range(2):
         nc.scalar.activation(
-            out=tab[:, :, a, 1, :].rearrange("p t (m e) -> p t m e", e=2),
-            in_=rest[:, 1, :, (1 - a) * HALF // 2 : (2 - a) * HALF // 2].unsqueeze(3).to_broadcast([P, T, HALF // 2, 2]),
+            out=tab[:, :, a, 1, :],
+            in_=rest[:, 1, :, (1 - a) * quarter : (2 - a) * quarter],
             func=ACT.Sin,
             scale=-two_pi if a == 0 else two_pi,
         )
@@ -130,7 +138,7 @@ def tile_spikinggroupedslidingattention_pa_kernel(tc, x, Wq, Wk, Wv, out_0, out_
         x_sb = xpool.tile([P, T, D], BF16)
         x_codes = xpool.tile([P, T, PASSES, P], U32, align_bytes=64)
         x_scales = xpool.tile([P, T, PASSES, P], U8, align_bytes=64)
-        tab = const.tile([P, T, 2, 2, HALF], F32)
+        tab = const.tile([P, T, 2, 2, NF // 2], F32)
         ident = const.tile([P, P], F32)
 
         raw = {}
@@ -222,13 +230,14 @@ def tile_spikinggroupedslidingattention_pa_kernel(tc, x, Wq, Wk, Wv, out_0, out_
                 result[n] = outp.tile([P, HPG, T, DH], F32, name="result")
             if t % 2 == 0:
                 prod[(n, t // 2)] = prodp.tile([P, HPG, 2, 2, 2, HALF], F32, name="pair")
+            shape = [P, HPG, 2, 2, NF // 2, 2]
             nc.vector.tensor_tensor(
-                out=prod[(n, t // 2)][:, :, t % 2],
+                out=prod[(n, t // 2)][:, :, t % 2].rearrange("p h a w (m e) -> p h a w m e", e=2),
                 in0=acc[(n, t)][:]
-                .rearrange("p (h a i) -> p h a i", a=2, i=HALF)
+                .rearrange("p (h a m e) -> p h a m e", a=2, e=2, m=NF // 2)
                 .unsqueeze(3)
-                .to_broadcast([P, HPG, 2, 2, HALF]),
-                in1=tab[:, t].unsqueeze(1).to_broadcast([P, HPG, 2, 2, HALF]),
+                .to_broadcast(shape),
+                in1=tab[:, t].unsqueeze(1).unsqueeze(5).to_broadcast(shape),
                 op=ALU.mult,
             )
 
@@ -277,53 +286,50 @@ def tile_spikinggroupedslidingattention_pa_kernel(tc, x, Wq, Wk, Wv, out_0, out_
             transpose_x(t)
             regroup_x(t)
 
-        for first, x_tiles in ((0, (0,)), (3, (1,)), (6, (2, 3))):
-            for u in range(first, first + 3):
-                if u < 8:
-                    load_unit(u)
+        for units, x_tiles in (((0, 1, 2), (0,)), ((3, 4), (1,)), ((5, 6, 7), (2, 3)), (range(8, RAW_BUFS), ())):
+            for u in units:
+                load_unit(u)
             for t in x_tiles:
                 load_x(t)
-        for u in range(8, RAW_BUFS):
-            load_unit(u)
         masks.make_identity(nc, ident[:])
 
         ctx.enter_context(tc.manual_schedule())
         rest = rope_angles(nc, const)
-        regroup(0)
         rope_tables(nc, rest, tab)
+        regroup(0)
         regroup(1)
-        regroup(2)
         quantise(0)
         quantise(1)
-        quantise(2)
-        regroup(3)
-        quantise(3)
-        regroup(4)
+        regroup(2)
         bring_x(0)
+        regroup(3)
+        quantise(2)
+        quantise(3)
+        quantise_x(0)
+        regroup(4)
+        bring_x(1)
         regroup(5)
         quantise(4)
-        quantise(5)
-        quantise_x(0)
-        regroup(6)
-        bring_x(1)
-        regroup(7)
-        quantise(6)
-        quantise(7)
         quantise_x(1)
-        bring_x(2)
-        bring_x(3)
+        quantise(5)
         multiply_tile(0, 0)
         multiply_tile(0, 1)
+        regroup(6)
+        bring_x(2)
+        bring_x(3)
+        regroup(7)
+        rotate_pair(0)
+        quantise(6)
+        quantise(7)
         regroup(8)
         quantise_x(2)
         quantise(8)
-        rotate_pair(0)
-        regroup(9)
-        regroup(10)
         quantise_x(3)
         multiply_tile(0, 2)
         multiply_tile(0, 3)
         multiply_group(1)
+        regroup(9)
+        regroup(10)
         rotate_pair(1)
         quantise(9)
         rotate_pair(2)

@@ -29,6 +29,8 @@ HPG = NCOL // DH
 N_GROUPS = 6
 N_UNITS = N_GROUPS * PASSES
 RAW_BUFS = 14
+V_HEADS = HPG // 2
+V_COLS = V_HEADS * DH
 VECTOR_UNITS = (0, 1, 3, 5, 7, 8, 10)
 
 FLOPS = 2 * S * D * (2048 + 512 + 512)
@@ -40,37 +42,31 @@ def rope_angles(nc, pool):
     nc.scalar.activation(out=warm[:, 1:2], in_=warm[:, 0:1], func=ACT.Sin)
 
     side = 8
-    half = side // 2
-    one = pool.tile([P, 1], F32)
-    nc.vector.memset(one[:], 1.0)
     rows = pool.tile([P, 2, side], F32)
-    for r, step, first in ((0, side, 1.0 / (2.0 * math.pi)), (1, 1, 1.0)):
-        for c in range(half):
+    nc.vector.memset(rows[:, :, 0:1], 1.0)
+    w = 1
+    while w < side:
+        for r, step in ((0, side), (1, 1)):
             nc.vector.tensor_scalar(
-                out=rows[:, r, c : c + 1],
-                in0=one[:],
-                scalar1=first * THETA ** (-c * step / NF),
+                out=rows[:, r, w : 2 * w],
+                in0=rows[:, r, 0:w],
+                scalar1=THETA ** (-w * step / NF),
                 scalar2=None,
                 op0=ALU.mult,
             )
-    for r, step in ((0, side), (1, 1)):
-        nc.vector.tensor_scalar(
-            out=rows[:, r, half:],
-            in0=rows[:, r, :half],
-            scalar1=THETA ** (-half * step / NF),
-            scalar2=None,
-            op0=ALU.mult,
-        )
+        w = 2 * w
 
     pos = pool.tile([P, T], I32)
     nc.gpsimd.iota(pos[:], pattern=[[1, T]], base=0, channel_multiplier=T)
 
     coarse = pool.tile([P, T, side], F32)
-    nc.vector.tensor_tensor(
+    nc.vector.scalar_tensor_tensor(
         out=coarse[:],
         in0=rows[:, 0].unsqueeze(1).to_broadcast([P, T, side]),
+        scalar=1.0 / (2.0 * math.pi),
         in1=pos[:].unsqueeze(2).to_broadcast([P, T, side]),
-        op=ALU.mult,
+        op0=ALU.mult,
+        op1=ALU.mult,
     )
     turns = pool.tile([P, T, NF], F32)
     nc.vector.tensor_tensor(
@@ -250,11 +246,12 @@ def tile_spikinggroupedslidingattention_pa_kernel(tc, x, Wq, Wk, Wv, out_0, out_
                 op=ALU.add,
             )
 
-        def store(n, t, count):
+        def store(n, t, count, heads=(0, HPG)):
             out_dram, h0 = groups[n][2:4]
+            first, end = heads
             nc.sync.dma_start(
-                out=out_dram.rearrange("b h (p t) i -> p (b h) t i", t=T)[:, h0 : h0 + HPG, t : t + count, :],
-                in_=result[n][:, :, t : t + count, :],
+                out=out_dram.rearrange("b h (p t) i -> p (b h) t i", t=T)[:, h0 + first : h0 + end, t : t + count, :],
+                in_=result[n][:, first:end, t : t + count, :],
             )
 
         def rotate_pair(pair):
@@ -276,11 +273,68 @@ def tile_spikinggroupedslidingattention_pa_kernel(tc, x, Wq, Wk, Wv, out_0, out_
             for t in range(T):
                 multiply_tile(n, t)
 
-        def empty(n, t, engine_copy):
-            if t == 0:
-                result[n] = outp.tile([P, HPG, T, DH], F32, name="result")
-            engine_copy(out=result[n][:, :, t, :], in_=acc[(n, t)][:].rearrange("p (h i) -> p h i", i=DH))
-            store(n, t, 1)
+        v_grouped = {}
+        v_mx = {}
+        v_acc = {}
+        last = N_GROUPS - 1
+
+        def regroup_v(g, half):
+            if half not in v_grouped:
+                v_grouped[half] = grpp.tile([P, PASSES, V_COLS * PACK], BF16, align_bytes=64, name="grouped")
+            src = raw[last * PASSES + g][:, :, half * V_COLS : (half + 1) * V_COLS]
+            nc.scalar.copy(
+                out=v_grouped[half][:, g, :].rearrange("p (c i j) -> p c j i", i=8, j=PACK),
+                in_=src.rearrange("p j (c i) -> p c j i", i=8),
+            )
+
+        def quantise_v(half, g, count):
+            if half not in v_mx:
+                w_codes = wcp.tile([P, PASSES, V_COLS], U32, align_bytes=64, name="w_codes")
+                w_scales = wcp.tile([P, PASSES, V_COLS], U8, align_bytes=64, name="w_scales")
+                v_mx[half] = (w_codes, w_scales)
+            w_codes, w_scales = v_mx[half]
+            nc.vector.quantize_mx(
+                out=w_codes[:, g : g + count, :].rearrange("p g c -> p (g c)").bitcast(FP8X4),
+                scales=w_scales[:, g : g + count, :].rearrange("p g c -> p (g c)"),
+                in_=v_grouped[half][:, g : g + count, :].rearrange("p g c -> p (g c)"),
+            )
+
+        def multiply_v(half, t, g, out):
+            w_codes, w_scales = v_mx[half]
+            nc.tensor.matmul_mx(
+                out=out,
+                lhsT=x_codes[:, t, g, :].bitcast(FP8X4),
+                lhsT_scale=x_scales[:, t, g, :],
+                rhs=w_codes[:, g, :].bitcast(FP8X4),
+                rhs_scale=w_scales[:, g, :],
+                start=(g == 0),
+                stop=(g == PASSES - 1),
+            )
+
+        def multiply_first_half():
+            for t in range(T):
+                if t % 2 == 0:
+                    v_acc[(0, t // 2)] = psum.tile([P, 2, V_COLS], F32, tag="bank", name="acc")
+                for g in range(PASSES):
+                    multiply_v(0, t, g, v_acc[(0, t // 2)][:, t % 2, :])
+
+        def multiply_second_half(g):
+            for t in range(T):
+                if g == 0:
+                    v_acc[(1, t)] = psum.tile([P, V_COLS], F32, tag="bank", name="acc")
+                multiply_v(1, t, g, v_acc[(1, t)][:])
+
+        def empty_first_half(pair):
+            nc.scalar.copy(
+                out=result[last][:, 0:V_HEADS, 2 * pair : 2 * pair + 2, :],
+                in_=v_acc[(0, pair)][:].rearrange("p t (h i) -> p h t i", i=DH),
+            )
+
+        def empty_second_half(t, engine_copy):
+            engine_copy(
+                out=result[last][:, V_HEADS:HPG, t, :],
+                in_=v_acc[(1, t)][:].rearrange("p (h i) -> p h i", i=DH),
+            )
 
         def bring_x(t):
             transpose_x(t)
@@ -319,8 +373,7 @@ def tile_spikinggroupedslidingattention_pa_kernel(tc, x, Wq, Wk, Wv, out_0, out_
         bring_x(3)
         regroup(7)
         rotate_pair(0)
-        quantise(6)
-        quantise(7)
+        quantise(6, 2)
         regroup(8)
         quantise_x(2)
         quantise(8)
@@ -333,34 +386,40 @@ def tile_spikinggroupedslidingattention_pa_kernel(tc, x, Wq, Wk, Wv, out_0, out_
         rotate_pair(1)
         quantise(9)
         rotate_pair(2)
-        for u in range(10, N_UNITS - 2, 2):
+        for u in range(10, last * PASSES, 2):
             if u > 10:
                 regroup(u)
             regroup(u + 1)
             quantise(u, 2)
-            n = u // PASSES
-            if n == N_GROUPS - 1:
-                for g in range(2):
-                    for t in range(T):
-                        multiply(n, t, g)
-            elif u % PASSES == 2:
-                multiply_group(n)
+            if u % PASSES == 2:
+                multiply_group(u // PASSES)
             rotate_pair(u // 2 - 2)
-        n = N_GROUPS - 2
-        regroup(N_UNITS - 2)
-        regroup(N_UNITS - 1)
-        quantise(N_UNITS - 2)
-        for t in range(T):
-            multiply(n + 1, t, 2)
+        result[last] = outp.tile([P, HPG, T, DH], F32, name="result")
+        for g in range(PASSES):
+            regroup_v(g, 0)
+        quantise_v(0, 0, 2)
+        rotate_pair(8)
+        quantise_v(0, 2, 2)
+        multiply_first_half()
+        n = last - 1
         products(n, 2)
-        quantise(N_UNITS - 1)
-        for t in range(T):
-            multiply(n + 1, t, 3)
-        add(nc.vector, n, 2, 1)
-        store(n, 2, 1)
         products(n, 3)
-        for t in range(T - 1):
-            empty(n + 1, t, nc.scalar.copy)
-        empty(n + 1, T - 1, nc.vector.tensor_copy)
-        add(nc.vector, n, 3, 1)
-        store(n, 3, 1)
+        regroup_v(0, 1)
+        regroup_v(1, 1)
+        quantise_v(1, 0, 2)
+        for g in range(2):
+            multiply_second_half(g)
+        add(nc.vector, n, 2, 2)
+        store(n, 2, 2)
+        regroup_v(2, 1)
+        empty_first_half(0)
+        regroup_v(3, 1)
+        empty_first_half(1)
+        store(last, 0, T, (0, V_HEADS))
+        for g in range(2, PASSES):
+            quantise_v(1, g, 1)
+            multiply_second_half(g)
+        for t in range(T):
+            empty_second_half(t, nc.scalar.copy if t % 2 == 0 else nc.vector.tensor_copy)
+            if t % 2 == 1:
+                store(last, t - 1, 2, (V_HEADS, HPG))

@@ -404,21 +404,20 @@ def tile_spikinggroupedslidingattention_pa_kernel(tc, x, Wq, Wk, Wv, out_0, out_
         n = last - 1
         products(n, 2)
         products(n, 3)
-        regroup_v(0, 1)
-        regroup_v(1, 1)
+        for g in range(PASSES):
+            regroup_v(g, 1)
         quantise_v(1, 0, 2)
         for g in range(2):
             multiply_second_half(g)
-        add(nc.vector, n, 2, 2)
-        store(n, 2, 2)
-        regroup_v(2, 1)
         empty_first_half(0)
-        regroup_v(3, 1)
         empty_first_half(1)
         store(last, 0, T, (0, V_HEADS))
-        for g in range(2, PASSES):
-            quantise_v(1, g, 1)
-            multiply_second_half(g)
+        quantise_v(1, 2, 1)
+        multiply_second_half(2)
+        add(nc.vector, n, 2, 2)
+        store(n, 2, 2)
+        quantise_v(1, 3, 1)
+        multiply_second_half(3)
         for t in range(T):
             empty_second_half(t, nc.scalar.copy if t % 2 == 0 else nc.vector.tensor_copy)
             if t % 2 == 1:

@@ -225,10 +225,10 @@ def tile_spikinggroupedslidingattention_pa_kernel(tc, x, Wq, Wk, Wv, out_0, out_
             if t == 0:
                 result[n] = outp.tile([P, HPG, T, DH], F32, name="result")
             if t % 2 == 0:
-                prod[(n, t // 2)] = prodp.tile([P, HPG, 2, 2, 2, HALF], F32, name="pair")
+                prod[(n, t // 2)] = prodp.tile([P, 2, 2, HPG, 2, HALF], F32, name="pair")
             shape = [P, HPG, 2, 2, NF // 2, 2]
             nc.vector.tensor_tensor(
-                out=prod[(n, t // 2)][:, :, t % 2].rearrange("p h a w (m e) -> p h a w m e", e=2),
+                out=prod[(n, t // 2)][:, :, t % 2].rearrange("p w h a (m e) -> p h a w m e", e=2),
                 in0=acc[(n, t)][:]
                 .rearrange("p (h a m e) -> p h a m e", a=2, e=2, m=NF // 2)
                 .unsqueeze(3)
@@ -240,9 +240,9 @@ def tile_spikinggroupedslidingattention_pa_kernel(tc, x, Wq, Wk, Wv, out_0, out_
         def add(engine, n, t, count):
             both = prod[(n, t // 2)][:, :, t % 2 : t % 2 + count]
             engine.tensor_tensor(
-                out=result[n][:, :, t : t + count, :].rearrange("p h t (a i) -> p h t a i", a=2),
-                in0=both[:, :, :, :, 0, :],
-                in1=both[:, :, :, ::-1, 1, :],
+                out=result[n][:, :, t : t + count, :].rearrange("p h t (a i) -> p t h a i", a=2),
+                in0=both[:, 0],
+                in1=both[:, 1, :, :, ::-1, :],
                 op=ALU.add,
             )
 

import math
from contextlib import ExitStack

import concourse.masks as masks
import concourse.mybir as mybir

F32 = mybir.dt.float32
BF16 = mybir.dt.bfloat16
I32 = mybir.dt.int32
U32 = mybir.dt.uint32
U8 = mybir.dt.uint8
FP8X4 = mybir.dt.float8_e4m3fn_x4
ALU = mybir.AluOpType
ACT = mybir.ActivationFunctionType

P = 128
S = 512
D = 2048
DH = 128
HALF = DH // 2
NF = DH // 2
THETA = 10000.0
T = S // P
PACK = 4
K_PASS = P * PACK
PASSES = D // K_PASS
NCOL = 512
HPG = NCOL // DH
N_GROUPS = 6
N_UNITS = N_GROUPS * PASSES
RAW_BUFS = 14
V_HEADS = HPG // 2
V_COLS = V_HEADS * DH
VECTOR_UNITS = (0, 1, 3, 5, 7, 8, 10)

FLOPS = 2 * S * D * (2048 + 512 + 512)


def rope_angles(nc, pool):
    warm = pool.tile([P, 2], F32)
    nc.vector.memset(warm[:, 0:1], 0.0)
    nc.scalar.activation(out=warm[:, 1:2], in_=warm[:, 0:1], func=ACT.Sin)

    side = 8
    rows = pool.tile([P, 2, side], F32)
    nc.vector.memset(rows[:, :, 0:1], 1.0)
    w = 1
    while w < side:
        for r, step in ((0, side), (1, 1)):
            nc.vector.tensor_scalar(
                out=rows[:, r, w : 2 * w],
                in0=rows[:, r, 0:w],
                scalar1=THETA ** (-w * step / NF),
                scalar2=None,
                op0=ALU.mult,
            )
        w = 2 * w

    pos = pool.tile([P, T], I32)
    nc.gpsimd.iota(pos[:], pattern=[[1, T]], base=0, channel_multiplier=T)

    coarse = pool.tile([P, T, side], F32)
    nc.vector.scalar_tensor_tensor(
        out=coarse[:],
        in0=rows[:, 0].unsqueeze(1).to_broadcast([P, T, side]),
        scalar=1.0 / (2.0 * math.pi),
        in1=pos[:].unsqueeze(2).to_broadcast([P, T, side]),
        op0=ALU.mult,
        op1=ALU.mult,
    )
    turns = pool.tile([P, T, NF], F32)
    nc.vector.tensor_tensor(
        out=turns[:].rearrange("p t (a b) -> p t a b", a=side),
        in0=coarse[:].unsqueeze(3).to_broadcast([P, T, side, side]),
        in1=rows[:, 1].unsqueeze(1).unsqueeze(1).to_broadcast([P, T, side, side]),
        op=ALU.mult,
    )
    whole = pool.tile([P, T, NF], I32)
    nc.vector.tensor_copy(out=whole[:], in_=turns[:])
    frac = pool.tile([P, 2, T, NF], F32)
    nc.vector.tensor_tensor(out=frac[:, 1], in0=turns[:], in1=whole[:], op=ALU.subtract)
    nc.vector.scalar_tensor_tensor(
        out=frac[:, 0], in0=turns[:], scalar=0.25, in1=whole[:], op0=ALU.add, op1=ALU.subtract
    )
    rest = pool.tile([P, 2, T, NF], F32)
    flat = "p a t m -> p (a t m)"
    nc.vector.scalar_tensor_tensor(
        out=rest[:].rearrange(flat),
        in0=frac[:].rearrange(flat),
        scalar=0.5,
        in1=frac[:].rearrange(flat),
        op0=ALU.is_gt,
        op1=ALU.subtract,
    )
    return rest


def rope_tables(nc, rest, tab):
    two_pi = 2.0 * math.pi
    quarter = NF // 2
    nc.scalar.activation(
        out=tab[:, :, :, 0, :],
        in_=rest[:, 0].rearrange("p t (a m) -> p t a m", a=2),
        func=ACT.Sin,
        scale=-two_pi,
    )
    for a in range(2):
        nc.scalar.activation(
            out=tab[:, :, a, 1, :],
            in_=rest[:, 1, :, (1 - a) * quarter : (2 - a) * quarter],
            func=ACT.Sin,
            scale=-two_pi if a == 0 else two_pi,
        )


def tile_spikinggroupedslidingattention_pa_kernel(tc, x, Wq, Wk, Wv, out_0, out_1, out_2):
    nc = tc.nc
    with ExitStack() as ctx:
        const = ctx.enter_context(tc.tile_pool(name="const", bufs=1))
        xpool = ctx.enter_context(tc.tile_pool(name="xpool", bufs=1))
        xgp = ctx.enter_context(tc.tile_pool(name="xgp", bufs=2))
        rawp = ctx.enter_context(tc.tile_pool(name="rawp", bufs=RAW_BUFS))
        grpp = ctx.enter_context(tc.tile_pool(name="grpp", bufs=4))
        wcp = ctx.enter_context(tc.tile_pool(name="wcp", bufs=3))
        prodp = ctx.enter_context(tc.tile_pool(name="prodp", bufs=3))
        outp = ctx.enter_context(tc.tile_pool(name="outp", bufs=3))
        psum = ctx.enter_context(tc.psum_pool(name="psum", bufs=8))

        groups = [(Wk, 0, out_1, 0, True)]
        for quarter in range(4):
            groups.append((Wq, quarter * NCOL, out_0, quarter * HPG, True))
        groups.append((Wv, 0, out_2, 0, False))

        x_sb = xpool.tile([P, T, D], BF16)
        x_codes = xpool.tile([P, T, PASSES, P], U32, align_bytes=64)
        x_scales = xpool.tile([P, T, PASSES, P], U8, align_bytes=64)
        tab = const.tile([P, T, 2, 2, NF // 2], F32)
        ident = const.tile([P, P], F32)

        raw = {}
        grouped = {}
        w_mx = {}
        acc = {}
        prod = {}
        result = {}
        x_t = {}
        x_grouped = {}

        def load_x(t):
            nc.sync.dma_start(out=x_sb[:, t, :], in_=x.rearrange("b (p t) k -> p (b t) k", t=T)[:, t, :])

        def load_unit(u):
            w_dram, c0 = groups[u // PASSES][0:2]
            g = u % PASSES
            raw[u] = rawp.tile([P, PACK, NCOL], BF16, name="raw")
            nc.sync.dma_start(
                out=raw[u][:],
                in_=w_dram[g * K_PASS : (g + 1) * K_PASS, c0 : c0 + NCOL].rearrange("(p j) c -> p j c", j=PACK),
            )

        def transpose_x(t):
            words = x_sb[:, t, :].bitcast(F32).rearrange("p (g q u) -> p g q u", g=PASSES, u=2)
            for half in range(2):
                x_t[(t, half)] = psum.tile([P, 4, P], F32, tag="bank", name="x_t")
                for g2 in range(2):
                    for u in range(2):
                        nc.tensor.transpose(x_t[(t, half)][:, 2 * g2 + u, :], words[:, 2 * half + g2, :, u], ident[:])

        def regroup_x(t):
            x_grouped[t] = xgp.tile([P, PASSES * P * PACK], BF16, align_bytes=64, name="x_grouped")
            dst = x_grouped[t][:].bitcast(F32).rearrange("p (g r u) -> p g r u", g=PASSES, u=2)
            for half in range(2):
                nc.scalar.copy(
                    out=dst[:, 2 * half : 2 * half + 2], in_=x_t[(t, half)][:].rearrange("p (g u) r -> p g r u", u=2)
                )

        def quantise_x(t):
            nc.vector.quantize_mx(
                out=x_codes[:, t].rearrange("p g r -> p (g r)").bitcast(FP8X4),
                scales=x_scales[:, t].rearrange("p g r -> p (g r)"),
                in_=x_grouped[t][:],
            )

        def regroup(u):
            if u // 2 not in grouped:
                grouped[u // 2] = grpp.tile([P, 2, NCOL * PACK], BF16, align_bytes=64, name="grouped")
            dst = grouped[u // 2][:, u % 2, :].rearrange("p (c i j) -> p c j i", i=8, j=PACK)
            src = raw[u][:].rearrange("p j (c i) -> p c j i", i=8)
            if u in VECTOR_UNITS:
                nc.vector.tensor_copy(out=dst, in_=src)
            else:
                nc.scalar.copy(out=dst, in_=src)
            if u + RAW_BUFS < N_UNITS:
                load_unit(u + RAW_BUFS)

        def quantise(u, count=1):
            n = u // PASSES
            g = u % PASSES
            if g == 0:
                w_codes = wcp.tile([P, PASSES, NCOL], U32, align_bytes=64, name="w_codes")
                w_scales = wcp.tile([P, PASSES, NCOL], U8, align_bytes=64, name="w_scales")
                w_mx[n] = (w_codes, w_scales)
            w_codes, w_scales = w_mx[n]
            nc.vector.quantize_mx(
                out=w_codes[:, g : g + count, :].rearrange("p g c -> p (g c)").bitcast(FP8X4),
                scales=w_scales[:, g : g + count, :].rearrange("p g c -> p (g c)"),
                in_=grouped[u // 2][:, u % 2 : u % 2 + count, :].rearrange("p e c -> p (e c)"),
            )

        def multiply(n, t, g):
            if g == 0:
                acc[(n, t)] = psum.tile([P, NCOL], F32, tag="bank", name="acc")
            w_codes, w_scales = w_mx[n]
            nc.tensor.matmul_mx(
                out=acc[(n, t)][:],
                lhsT=x_codes[:, t, g, :].bitcast(FP8X4),
                lhsT_scale=x_scales[:, t, g, :],
                rhs=w_codes[:, g, :].bitcast(FP8X4),
                rhs_scale=w_scales[:, g, :],
                start=(g == 0),
                stop=(g == PASSES - 1),
            )

        def products(n, t):
            if t == 0:
                result[n] = outp.tile([P, HPG, T, DH], F32, name="result")
            if t % 2 == 0:
                prod[(n, t // 2)] = prodp.tile([P, 2, 2, HPG, 2, HALF], F32, name="pair")
            shape = [P, HPG, 2, 2, NF // 2, 2]
            nc.vector.tensor_tensor(
                out=prod[(n, t // 2)][:, :, t % 2].rearrange("p w h a (m e) -> p h a w m e", e=2),
                in0=acc[(n, t)][:]
                .rearrange("p (h a m e) -> p h a m e", a=2, e=2, m=NF // 2)
                .unsqueeze(3)
                .to_broadcast(shape),
                in1=tab[:, t].unsqueeze(1).unsqueeze(5).to_broadcast(shape),
                op=ALU.mult,
            )

        def add(engine, n, t, count):
            both = prod[(n, t // 2)][:, :, t % 2 : t % 2 + count]
            engine.tensor_tensor(
                out=result[n][:, :, t : t + count, :].rearrange("p h t (a i) -> p t h a i", a=2),
                in0=both[:, 0],
                in1=both[:, 1, :, :, ::-1, :],
                op=ALU.add,
            )

        def store(n, t, count, heads=(0, HPG)):
            out_dram, h0 = groups[n][2:4]
            first, end = heads
            nc.sync.dma_start(
                out=out_dram.rearrange("b h (p t) i -> p (b h) t i", t=T)[:, h0 + first : h0 + end, t : t + count, :],
                in_=result[n][:, first:end, t : t + count, :],
            )

        def rotate_pair(pair):
            n = pair // 2
            t = 2 * (pair % 2)
            products(n, t)
            products(n, t + 1)
            add(nc.gpsimd, n, t, 2)
            if n == N_GROUPS - 2:
                store(n, t, 2)
            elif t > 0:
                store(n, 0, T)

        def multiply_tile(n, t):
            for g in range(PASSES):
                multiply(n, t, g)

        def multiply_group(n):
            for t in range(T):
                multiply_tile(n, t)

        v_grouped = {}
        v_mx = {}
        v_acc = {}
        last = N_GROUPS - 1

        def regroup_v(g, half):
            if half not in v_grouped:
                v_grouped[half] = grpp.tile([P, PASSES, V_COLS * PACK], BF16, align_bytes=64, name="grouped")
            src = raw[last * PASSES + g][:, :, half * V_COLS : (half + 1) * V_COLS]
            nc.scalar.copy(
                out=v_grouped[half][:, g, :].rearrange("p (c i j) -> p c j i", i=8, j=PACK),
                in_=src.rearrange("p j (c i) -> p c j i", i=8),
            )

        def quantise_v(half, g, count):
            if half not in v_mx:
                w_codes = wcp.tile([P, PASSES, V_COLS], U32, align_bytes=64, name="w_codes")
                w_scales = wcp.tile([P, PASSES, V_COLS], U8, align_bytes=64, name="w_scales")
                v_mx[half] = (w_codes, w_scales)
            w_codes, w_scales = v_mx[half]
            nc.vector.quantize_mx(
                out=w_codes[:, g : g + count, :].rearrange("p g c -> p (g c)").bitcast(FP8X4),
                scales=w_scales[:, g : g + count, :].rearrange("p g c -> p (g c)"),
                in_=v_grouped[half][:, g : g + count, :].rearrange("p g c -> p (g c)"),
            )

        def multiply_v(half, t, g, out):
            w_codes, w_scales = v_mx[half]
            nc.tensor.matmul_mx(
                out=out,
                lhsT=x_codes[:, t, g, :].bitcast(FP8X4),
                lhsT_scale=x_scales[:, t, g, :],
                rhs=w_codes[:, g, :].bitcast(FP8X4),
                rhs_scale=w_scales[:, g, :],
                start=(g == 0),
                stop=(g == PASSES - 1),
            )

        def multiply_first_half():
            for t in range(T):
                if t % 2 == 0:
                    v_acc[(0, t // 2)] = psum.tile([P, 2, V_COLS], F32, tag="bank", name="acc")
                for g in range(PASSES):
                    multiply_v(0, t, g, v_acc[(0, t // 2)][:, t % 2, :])

        def multiply_second_half(g):
            for t in range(T):
                if g == 0:
                    v_acc[(1, t)] = psum.tile([P, V_COLS], F32, tag="bank", name="acc")
                multiply_v(1, t, g, v_acc[(1, t)][:])

        def empty_first_half(pair):
            nc.scalar.copy(
                out=result[last][:, 0:V_HEADS, 2 * pair : 2 * pair + 2, :],
                in_=v_acc[(0, pair)][:].rearrange("p t (h i) -> p h t i", i=DH),
            )

        def empty_second_half(t, engine_copy):
            engine_copy(
                out=result[last][:, V_HEADS:HPG, t, :],
                in_=v_acc[(1, t)][:].rearrange("p (h i) -> p h i", i=DH),
            )

        def bring_x(t):
            transpose_x(t)
            regroup_x(t)

        for units, x_tiles in (((0, 1, 2), (0,)), ((3, 4), (1,)), ((5, 6, 7), (2, 3)), (range(8, RAW_BUFS), ())):
            for u in units:
                load_unit(u)
            for t in x_tiles:
                load_x(t)
        masks.make_identity(nc, ident[:])

        ctx.enter_context(tc.manual_schedule())
        rest = rope_angles(nc, const)
        rope_tables(nc, rest, tab)
        regroup(0)
        regroup(1)
        quantise(0)
        quantise(1)
        regroup(2)
        bring_x(0)
        regroup(3)
        quantise(2)
        quantise(3)
        quantise_x(0)
        regroup(4)
        bring_x(1)
        regroup(5)
        quantise(4)
        quantise_x(1)
        quantise(5)
        multiply_tile(0, 0)
        multiply_tile(0, 1)
        regroup(6)
        bring_x(2)
        bring_x(3)
        regroup(7)
        rotate_pair(0)
        quantise(6, 2)
        regroup(8)
        quantise_x(2)
        quantise(8)
        quantise_x(3)
        multiply_tile(0, 2)
        multiply_tile(0, 3)
        multiply_group(1)
        regroup(9)
        regroup(10)
        rotate_pair(1)
        quantise(9)
        rotate_pair(2)
        for u in range(10, last * PASSES, 2):
            if u > 10:
                regroup(u)
            regroup(u + 1)
            quantise(u, 2)
            if u % PASSES == 2:
                multiply_group(u // PASSES)
            rotate_pair(u // 2 - 2)
        result[last] = outp.tile([P, HPG, T, DH], F32, name="result")
        for g in range(PASSES):
            regroup_v(g, 0)
        quantise_v(0, 0, 2)
        rotate_pair(8)
        quantise_v(0, 2, 2)
        multiply_first_half()
        n = last - 1
        products(n, 2)
        products(n, 3)
        for g in range(PASSES):
            regroup_v(g, 1)
        quantise_v(1, 0, 2)
        for g in range(2):
            multiply_second_half(g)
        empty_first_half(0)
        empty_first_half(1)
        store(last, 0, T, (0, V_HEADS))
        quantise_v(1, 2, 1)
        multiply_second_half(2)
        add(nc.vector, n, 2, 2)
        store(n, 2, 2)
        quantise_v(1, 3, 1)
        multiply_second_half(3)
        for t in range(T):
            empty_second_half(t, nc.scalar.copy if t % 2 == 0 else nc.vector.tensor_copy)
            if t % 2 == 1:
                store(last, t - 1, 2, (V_HEADS, HPG))
